import numpy as np
import ml_dtypes


def mxq(x, axis, fmt="e4m3"):
    dtype, down = {"e4m3": (ml_dtypes.float8_e4m3fn, 7), "e5m2": (ml_dtypes.float8_e5m2, 14)}[fmt]
    v = np.moveaxis(np.asarray(x, np.float32).astype(ml_dtypes.bfloat16).astype(np.float64), axis, -1)
    blocks = v.reshape(v.shape[:-1] + (-1, 32))
    amax = np.abs(blocks).max(-1, keepdims=True)
    byte = np.maximum(np.where(amax > 0, np.frexp(amax)[1] - 1 + 127, 0) - down, 1)
    scale = np.exp2(byte - 127.0)
    codes = (blocks / scale).astype(np.float32).astype(dtype).astype(np.float64)
    return np.moveaxis((codes * scale).reshape(v.shape), -1, axis)


WIDE = False


def mx_kscale(k):
    if not WIDE:
        return np.ones(k)
    levels = np.array([10, -10, 5, -5, 0])
    a = np.random.permutation(np.resize(levels, k // 512 * 4)).reshape(k // 512, 4)
    idx = np.arange(k)
    return np.exp2(a[idx // 512, idx % 128 // 32])


BF16 = ml_dtypes.bfloat16


def bf(x):
    return np.asarray(x, np.float32).astype(BF16)


def f64(x):
    return np.asarray(x).astype(np.float64)


NM, B, IN, H1, H2, OUT = 8, 128, 512, 512, 512, 128
LS_LO, LS_HI = -20.0, 4.0


def fnoise(ei, ej):
    return np.sign(ei) * np.sign(ej) * np.sqrt(np.abs(ei)) * np.sqrt(np.abs(ej))


def plin(xq, w, b):
    y = xq.transpose(1, 0, 2) @ mxq(f64(w), 2, 'e4m3').transpose(0, 2, 1)
    return y.transpose(1, 0, 2) + f64(b)[None]


def setup_inputs():
    k = mx_kscale(IN)
    return {'s': bf(np.random.standard_normal((B, NM, IN)) * k),
            'ei1': bf(np.random.standard_normal((B, NM, 1))),
            'ej1': bf(np.random.standard_normal((1, NM, H1))),
            'w11': bf(np.random.standard_normal((NM, H1, IN)) / np.sqrt(IN) / k),
            'b11': bf(np.random.standard_normal((NM, H1)) * 0.3),
            'w12': bf(np.random.standard_normal((NM, H1, IN)) * 1.2 / np.sqrt(IN) / k),
            'b12': bf(np.random.standard_normal((NM, H1)) * 0.3)}


def reference(s, ei1, ej1, w11, b11, w12, b12):
    sq = mxq(f64(s), 2, 'e4m3')
    mu = plin(sq, w11, b11)
    log_sigma = np.clip(plin(sq, w12, b12), LS_LO, LS_HI)
    return np.maximum(mu + fnoise(f64(ei1), f64(ej1)) * np.exp(log_sigma), 0.0)

@@ -1,0 +1,217 @@
+import concourse.mybir as mybir
+from concourse.masks import make_identity
+
+F32 = mybir.dt.float32
+BF16 = mybir.dt.bfloat16
+U32 = mybir.dt.uint32
+U8 = mybir.dt.uint8
+I32 = mybir.dt.int32
+FP8X4 = mybir.dt.float8_e4m3fn_x4
+ALU = mybir.AluOpType
+ACT = mybir.ActivationFunctionType
+
+P = 128
+NM = 8
+K = 512
+H = 512
+NT = H // P
+FLOPS = 2 * 2 * P * NM * K * H
+PIN = False
+
+
+def tile_skill_net_pa_kernel(tc, s, ei1, ej1, w11, b11, w12, b12, out):
+    nc = tc.nc
+    with tc.tile_pool(name="const", bufs=1) as const, tc.tile_pool(name="raw", bufs=1) as raw, tc.tile_pool(
+        name="work", bufs=2
+    ) as work, tc.psum_pool(name="pst", bufs=4) as pst, tc.psum_pool(name="psx", bufs=2) as psx, tc.psum_pool(
+        name="pso", bufs=2
+    ) as pso:
+        s_sb = raw.tile([P, NM * K], BF16)
+        w_sb = [[None] * NM, [None] * NM]
+        vecs = const.tile([P, H], BF16)
+        nc.vector.memset(vecs[:].bitcast(I32), 0)
+        ei_sb = const.tile([P, NM], BF16)
+        nc.scalar.dma_start(out=vecs[0:8, :], in_=b11)
+        nc.scalar.dma_start(out=vecs[8:16, :], in_=b12)
+        nc.scalar.dma_start(out=vecs[16:24, :], in_=ej1.rearrange("o j l -> (o j) l"))
+        nc.scalar.dma_start(out=ei_sb[:], in_=ei1.rearrange("i j o -> i (j o)"))
+        s_flat = s.rearrange("i j k -> i (j k)")
+        half = NM * K // 2
+
+        def load_w(j):
+            for w, src in ((1, w12), (0, w11)):
+                t_w = raw.tile([P, NT * K], BF16, name="w%d_%d" % (w, j))
+                nc.sync.dma_start(out=t_w[:], in_=src[j].rearrange("(p t) k -> p (t k)", t=NT))
+                w_sb[w][j] = t_w
+
+        nc.sync.dma_start(out=s_sb[:, 0:half], in_=s_flat[:, 0:half])
+        load_w(0)
+        load_w(1)
+        nc.sync.dma_start(out=s_sb[:, half:], in_=s_flat[:, half:])
+        for j in range(2, NM):
+            load_w(j)
+
+        ident = const.tile([P, P], F32)
+        make_identity(nc, ident[:])
+
+        vecf = const.tile([P, NT * P], F32)
+        nc.vector.tensor_copy(
+            out=vecf[:].rearrange("r (t p) -> r t p", t=NT), in_=vecs[:].rearrange("r (p t) -> r t p", t=NT)
+        )
+        vt = pst.tile([P, NT * P], F32, tag="tp")
+        for t in range(NT):
+            nc.tensor.transpose(vt[:, P * t : P * t + P], vecf[:, P * t : P * t + P], ident[:])
+        bias = const.tile([P, NT * 16], F32)
+        nc.vector.tensor_copy(
+            out=bias[:].rearrange("p (t r) -> p t r", t=NT), in_=vt[:].rearrange("p (t r) -> p t r", t=NT)[:, :, 0:16]
+        )
+        ee = const.tile([P, 40], F32)
+        nc.vector.tensor_copy(
+            out=ee[:, 0:32].rearrange("p (t r) -> p t r", t=NT),
+            in_=vt[:].rearrange("p (t r) -> p t r", t=NT)[:, :, 16:24],
+        )
+        nc.vector.tensor_copy(out=ee[:, 32:40], in_=ei_sb[:])
+        mag = const.tile([P, 40], F32)
+        nc.vector.scalar_tensor_tensor(out=mag[:], in0=ee[:], scalar=-1.0, in1=ee[:], op0=ALU.mult, op1=ALU.max)
+        nc.vector.tensor_scalar_max(out=mag[:], in0=mag[:], scalar1=2.0 ** -116)
+        root = const.tile([P, 40], F32)
+        nc.scalar.activation(out=root[:], in_=mag[:], func=ACT.Sqrt)
+        sgn = const.tile([P, 40], F32)
+        nc.scalar.activation(out=sgn[:], in_=ee[:], func=ACT.Sign)
+        f = const.tile([P, 40], F32)
+        nc.vector.tensor_mul(out=f[:], in0=root[:], in1=sgn[:])
+        bounds = const.tile([P, 2], F32)
+        nc.vector.memset(bounds[:, 0:1], -20.0)
+        nc.vector.memset(bounds[:, 1:2], 4.0)
+        ebounds = const.tile([P, 2], F32)
+        nc.scalar.activation(out=ebounds[:], in_=bounds[:], func=ACT.Exp)
+        rep = const.tile([P, NM * P], F32)
+        nc.vector.tensor_copy(
+            out=rep[:].rearrange("i (j c) -> i j c", j=NM), in_=f[:, 32:40].unsqueeze(2).to_broadcast([P, NM, P])
+        )
+        fi_all = const.tile([P, NM * P], F32)
+        for hh in range(2):
+            ft = pst.tile([P, 4 * P], F32, tag="tp")
+            for a in range(4):
+                c = 4 * hh + a
+                nc.tensor.transpose(ft[:, P * a : P * a + P], rep[:, P * c : P * c + P], ident[:])
+            nc.vector.tensor_copy(out=fi_all[:, 512 * hh : 512 * hh + 512], in_=ft[:])
+
+        s_codes = [None, None]
+        s_scl = [None, None]
+        w_codes = {}
+        w_scl = {}
+        acc = {}
+        o_sb = {}
+
+        def flip(src32, engine_copy):
+            g = work.tile([P, 2048], BF16, align_bytes=64, tag="g", bufs=4)
+            g32 = g[:].bitcast(F32)
+            for h in range(2):
+                tp = pst.tile([P, 512], F32, tag="tp")
+                for a in range(2):
+                    for u in range(2):
+                        c = 256 * (2 * h + a) + P * u
+                        nc.tensor.transpose(tp[:, 256 * a + P * u : 256 * a + P * u + P], src32[:, c : c + P], ident[:])
+                engine_copy(
+                    out=g32[:, 512 * h : 512 * h + 512].rearrange("q (a p u) -> q a p u", a=2, u=2),
+                    in_=tp[:].rearrange("q (a u p) -> q a p u", a=2, u=2),
+                )
+            return g
+
+        def quant(g, tag, bufs):
+            codes = work.tile([P, 512], U32, align_bytes=64, tag="c" + tag, bufs=bufs)
+            scl = work.tile([P, 512], U8, align_bytes=64, tag="s" + tag, bufs=bufs)
+            nc.vector.quantize_mx(out=codes[:].bitcast(FP8X4), scales=scl[:], in_=g[:])
+            return codes, scl
+
+        def prep_s(hs):
+            g = flip(s_sb[:].bitcast(F32)[:, 1024 * hs : 1024 * hs + 1024], nc.vector.tensor_copy)
+            s_codes[hs], s_scl[hs] = quant(g, "s", 2)
+
+        def prep_w(j):
+            for w in (1, 0):
+                g = flip(w_sb[w][j][:].bitcast(F32), nc.scalar.copy)
+                w_codes[(w, j)], w_scl[(w, j)] = quant(g, "w", 4)
+
+        def mx(j):
+            col = P * (j % 4)
+            for w in (1, 0):
+                ps = psx.tile([P, 512], F32, tag="mx")
+                for t in range(NT):
+                    nc.tensor.matmul_mx(
+                        out=ps[:, P * t : P * t + P],
+                        lhsT=w_codes[(w, j)][:, P * t : P * t + P].bitcast(FP8X4),
+                        lhsT_scale=w_scl[(w, j)][:, P * t : P * t + P],
+                        rhs=s_codes[j // 4][:, col : col + P].bitcast(FP8X4),
+                        rhs_scale=s_scl[j // 4][:, col : col + P],
+                        start=True,
+                        stop=True,
+                    )
+                acc[(w, j)] = ps
+
+        def epilogue(j):
+            e = work.tile([P, 512], F32, tag="e")
+            for t in range(NT):
+                nc.scalar.activation(
+                    out=e[:, P * t : P * t + P],
+                    in_=acc[(1, j)][:, P * t : P * t + P],
+                    func=ACT.Exp,
+                    bias=bias[:, 16 * t + 8 + j : 16 * t + 9 + j],
+                    scale=1.0,
+                )
+            a_sb = work.tile([P, 512], F32, tag="a")
+            nc.vector.tensor_scalar(
+                out=a_sb[:], in0=e[:], scalar1=ebounds[:, 0:1], scalar2=ebounds[:, 1:2], op0=ALU.max, op1=ALU.min
+            )
+            z = work.tile([P, 512], F32, tag="z")
+            o = work.tile([P, 512], F32, tag="o")
+            for t in range(NT):
+                nc.vector.scalar_tensor_tensor(
+                    out=z[:, P * t : P * t + P],
+                    in0=a_sb[:, P * t : P * t + P],
+                    scalar=f[:, 8 * t + j : 8 * t + j + 1],
+                    in1=fi_all[:, P * j : P * j + P],
+                    op0=ALU.mult,
+                    op1=ALU.mult,
+                )
+            for t in range(NT):
+                nc.vector.scalar_tensor_tensor(
+                    out=o[:, P * t : P * t + P],
+                    in0=acc[(0, j)][:, P * t : P * t + P],
+                    scalar=bias[:, 16 * t + j : 16 * t + j + 1],
+                    in1=z[:, P * t : P * t + P],
+                    op0=ALU.add,
+                    op1=ALU.add,
+                )
+            o_sb[j] = o
+
+        def finish(j):
+            ot = pso.tile([P, 512], F32, tag="ot")
+            for t in range(NT):
+                nc.tensor.transpose(ot[:, P * t : P * t + P], o_sb[j][:, P * t : P * t + P], ident[:])
+            r = work.tile([P, 512], F32, tag="r", bufs=3)
+            nc.scalar.activation(
+                out=r[:].rearrange("i (p t) -> i p t", t=NT), in_=ot[:].rearrange("i (t p) -> i p t", t=NT), func=ACT.Relu
+            )
+            nc.sync.dma_start(out=out[:, j, :], in_=r[:])
+
+        def body():
+            prep_s(0)
+            prep_w(0)
+            for i in range(NM):
+                if i + 1 < NM:
+                    prep_w(i + 1)
+                if i == 2:
+                    prep_s(1)
+                if i >= 1:
+                    finish(i - 1)
+                mx(i)
+                epilogue(i)
+            finish(NM - 1)
+
+        if PIN:
+            with tc.manual_schedule():
+                body()
+        else:
+            body()

@@ -16,18 +16,16 @@ K = 512
 H = 512
 NT = H // P
 FLOPS = 2 * 2 * P * NM * K * H
-PIN = False
+LS, MU = 1, 0
 
 
 def tile_skill_net_pa_kernel(tc, s, ei1, ej1, w11, b11, w12, b12, out):
     nc = tc.nc
     with tc.tile_pool(name="const", bufs=1) as const, tc.tile_pool(name="raw", bufs=1) as raw, tc.tile_pool(
         name="work", bufs=2
-    ) as work, tc.psum_pool(name="pst", bufs=4) as pst, tc.psum_pool(name="psx", bufs=2) as psx, tc.psum_pool(
-        name="pso", bufs=2
-    ) as pso:
-        s_sb = raw.tile([P, NM * K], BF16)
-        w_sb = [[None] * NM, [None] * NM]
+    ) as work, tc.psum_pool(name="pst", bufs=4) as pst, tc.psum_pool(name="psx", bufs=3) as psx, tc.psum_pool(
+        name="pso", bufs=1
+    ) as pso, tc.manual_schedule():
         vecs = const.tile([P, H], BF16)
         nc.vector.memset(vecs[:].bitcast(I32), 0)
         ei_sb = const.tile([P, NM], BF16)
@@ -35,24 +33,41 @@ def tile_skill_net_pa_kernel(tc, s, ei1, ej1, w11, b11, w12, b12, out):
         nc.scalar.dma_start(out=vecs[8:16, :], in_=b12)
         nc.scalar.dma_start(out=vecs[16:24, :], in_=ej1.rearrange("o j l -> (o j) l"))
         nc.scalar.dma_start(out=ei_sb[:], in_=ei1.rearrange("i j o -> i (j o)"))
+
+        s_sb = raw.tile([P, NM * K], BF16)
         s_flat = s.rearrange("i j k -> i (j k)")
-        half = NM * K // 2
+        w_dram = {LS: w12, MU: w11}
+        w_sb = {}
+        for j in range(NM):
+            for w in (LS, MU):
+                w_sb[(w, j)] = raw.tile([P, NT * K], BF16, name="w%d_%d" % (w, j))
 
-        def load_w(j):
-            for w, src in ((1, w12), (0, w11)):
-                t_w = raw.tile([P, NT * K], BF16, name="w%d_%d" % (w, j))
-                nc.sync.dma_start(out=t_w[:], in_=src[j].rearrange("(p t) k -> p (t k)", t=NT))
-                w_sb[w][j] = t_w
+        def load_w(w, j, c0, c1):
+            nc.sync.dma_start(
+                out=w_sb[(w, j)][:, c0:c1], in_=w_dram[w][j].rearrange("(p t) k -> p (t k)", t=NT)[:, c0:c1]
+            )
 
-        nc.sync.dma_start(out=s_sb[:, 0:half], in_=s_flat[:, 0:half])
-        load_w(0)
-        load_w(1)
-        nc.sync.dma_start(out=s_sb[:, half:], in_=s_flat[:, half:])
-        for j in range(2, NM):
-            load_w(j)
+        def load_s(c):
+            nc.sync.dma_start(out=s_sb[:, 2 * K * c : 2 * K * (c + 1)], in_=s_flat[:, 2 * K * c : 2 * K * (c + 1)])
+
+        load_w(LS, 0, 0, 2 * K)
+        load_w(LS, 0, 2 * K, 4 * K)
+        load_s(0)
+        load_w(MU, 0, 0, 4 * K)
+        for j in range(1, NM):
+            load_w(LS, j, 0, 4 * K)
+            load_w(MU, j, 0, 4 * K)
+            if j % 2 == 1 and j < 7:
+                load_s((j + 1) // 2)
 
         ident = const.tile([P, P], F32)
         make_identity(nc, ident[:])
+
+        bounds = const.tile([P, 2], F32)
+        nc.vector.memset(bounds[:, 0:1], -20.0)
+        nc.vector.memset(bounds[:, 1:2], 4.0)
+        warm = const.tile([P, 1], F32)
+        nc.scalar.activation(out=warm[:], in_=bounds[:, 1:2], func=ACT.Sqrt)
 
         vecf = const.tile([P, NT * P], F32)
         nc.vector.tensor_copy(
@@ -61,108 +76,112 @@ def tile_skill_net_pa_kernel(tc, s, ei1, ej1, w11, b11, w12, b12, out):
         vt = pst.tile([P, NT * P], F32, tag="tp")
         for t in range(NT):
             nc.tensor.transpose(vt[:, P * t : P * t + P], vecf[:, P * t : P * t + P], ident[:])
+        vt3 = vt[:].rearrange("p (t r) -> p t r", t=NT)
         bias = const.tile([P, NT * 16], F32)
-        nc.vector.tensor_copy(
-            out=bias[:].rearrange("p (t r) -> p t r", t=NT), in_=vt[:].rearrange("p (t r) -> p t r", t=NT)[:, :, 0:16]
-        )
+        nc.vector.tensor_copy(out=bias[:].rearrange("p (t r) -> p t r", t=NT), in_=vt3[:, :, 0:16])
         ee = const.tile([P, 40], F32)
-        nc.vector.tensor_copy(
-            out=ee[:, 0:32].rearrange("p (t r) -> p t r", t=NT),
-            in_=vt[:].rearrange("p (t r) -> p t r", t=NT)[:, :, 16:24],
-        )
+        nc.vector.tensor_copy(out=ee[:, 0:32].rearrange("p (t r) -> p t r", t=NT), in_=vt3[:, :, 16:24])
         nc.vector.tensor_copy(out=ee[:, 32:40], in_=ei_sb[:])
         mag = const.tile([P, 40], F32)
         nc.vector.scalar_tensor_tensor(out=mag[:], in0=ee[:], scalar=-1.0, in1=ee[:], op0=ALU.mult, op1=ALU.max)
         nc.vector.tensor_scalar_max(out=mag[:], in0=mag[:], scalar1=2.0 ** -116)
+        neg = const.tile([P, 40], F32)
+        nc.vector.tensor_single_scalar(out=neg[:], in_=ee[:], scalar=0.0, op=ALU.is_lt)
+        sgn = const.tile([P, 40], F32)
+        nc.vector.scalar_tensor_tensor(out=sgn[:], in0=ee[:], scalar=0.0, in1=neg[:], op0=ALU.is_gt, op1=ALU.subtract)
         root = const.tile([P, 40], F32)
         nc.scalar.activation(out=root[:], in_=mag[:], func=ACT.Sqrt)
-        sgn = const.tile([P, 40], F32)
-        nc.scalar.activation(out=sgn[:], in_=ee[:], func=ACT.Sign)
-        f = const.tile([P, 40], F32)
-        nc.vector.tensor_mul(out=f[:], in0=root[:], in1=sgn[:])
-        bounds = const.tile([P, 2], F32)
-        nc.vector.memset(bounds[:, 0:1], -20.0)
-        nc.vector.memset(bounds[:, 1:2], 4.0)
         ebounds = const.tile([P, 2], F32)
         nc.scalar.activation(out=ebounds[:], in_=bounds[:], func=ACT.Exp)
+        f = const.tile([P, 40], F32)
         rep = const.tile([P, NM * P], F32)
-        nc.vector.tensor_copy(
-            out=rep[:].rearrange("i (j c) -> i j c", j=NM), in_=f[:, 32:40].unsqueeze(2).to_broadcast([P, NM, P])
-        )
         fi_all = const.tile([P, NM * P], F32)
-        for hh in range(2):
-            ft = pst.tile([P, 4 * P], F32, tag="tp")
-            for a in range(4):
-                c = 4 * hh + a
-                nc.tensor.transpose(ft[:, P * a : P * a + P], rep[:, P * c : P * c + P], ident[:])
-            nc.vector.tensor_copy(out=fi_all[:, 512 * hh : 512 * hh + 512], in_=ft[:])
 
-        s_codes = [None, None]
-        s_scl = [None, None]
-        w_codes = {}
-        w_scl = {}
+        banks = {}
+        grouped = {}
+        codes = {}
+        scales = {}
         acc = {}
-        o_sb = {}
+        sb = {}
 
-        def flip(src32, engine_copy):
-            g = work.tile([P, 2048], BF16, align_bytes=64, tag="g", bufs=4)
-            g32 = g[:].bitcast(F32)
-            for h in range(2):
-                tp = pst.tile([P, 512], F32, tag="tp")
-                for a in range(2):
-                    for u in range(2):
-                        c = 256 * (2 * h + a) + P * u
-                        nc.tensor.transpose(tp[:, 256 * a + P * u : 256 * a + P * u + P], src32[:, c : c + P], ident[:])
-                engine_copy(
-                    out=g32[:, 512 * h : 512 * h + 512].rearrange("q (a p u) -> q a p u", a=2, u=2),
-                    in_=tp[:].rearrange("q (a u p) -> q a p u", a=2, u=2),
+        def flip(key, src32, n):
+            tp = pst.tile([P, 512], F32, tag="tp")
+            for a in range(n):
+                nc.tensor.transpose(tp[:, P * a : P * a + P], src32[:, P * a : P * a + P], ident[:])
+            banks[key] = tp
+
+        def t_w(j, w, h):
+            flip((w, j, h), w_sb[(w, j)][:].bitcast(F32)[:, 512 * h : 512 * h + 512], 4)
+
+        def e_w(j, w, h, copy):
+            if h == 0:
+                grouped[(w, j)] = work.tile([P, 2048], BF16, align_bytes=64, tag="g", bufs=4, name="g")
+            copy(
+                out=grouped[(w, j)][:].bitcast(F32)[:, 512 * h : 512 * h + 512].rearrange(
+                    "q (a p u) -> q a p u", a=2, u=2
+                ),
+                in_=banks[(w, j, h)][:].rearrange("q (a u p) -> q a p u", a=2, u=2),
+            )
+
+        def q_w(j, w):
+            codes[(w, j)] = work.tile([P, 512], U32, align_bytes=64, tag="cw", bufs=4, name="cw")
+            scales[(w, j)] = work.tile([P, 512], U8, align_bytes=64, tag="sw", bufs=4, name="sw")
+            nc.vector.quantize_mx(
+                out=codes[(w, j)][:].bitcast(FP8X4), scales=scales[(w, j)][:], in_=grouped[(w, j)][:]
+            )
+
+        def t_s(j):
+            flip(("s", j), s_sb[:].bitcast(F32)[:, 256 * j : 256 * j + 256], 2)
+
+        def e_s(j):
+            grouped[("s", j)] = work.tile([P, 512], BF16, align_bytes=64, tag="gs", bufs=3, name="gs")
+            nc.vector.tensor_copy(
+                out=grouped[("s", j)][:].bitcast(F32).rearrange("q (p u) -> q p u", u=2),
+                in_=banks[("s", j)][:, 0:256].rearrange("q (u p) -> q p u", u=2),
+            )
+
+        def q_s(j):
+            codes[("s", j)] = work.tile([P, P], U32, align_bytes=64, tag="cs", bufs=3, name="cs")
+            scales[("s", j)] = work.tile([P, P], U8, align_bytes=64, tag="ss", bufs=3, name="ss")
+            nc.vector.quantize_mx(
+                out=codes[("s", j)][:].bitcast(FP8X4), scales=scales[("s", j)][:], in_=grouped[("s", j)][:]
+            )
+
+        def mx(j, w):
+            ps = psx.tile([P, 512], F32, tag="mx")
+            for t in range(NT):
+                nc.tensor.matmul_mx(
+                    out=ps[:, P * t : P * t + P],
+                    lhsT=codes[(w, j)][:, P * t : P * t + P].bitcast(FP8X4),
+                    lhsT_scale=scales[(w, j)][:, P * t : P * t + P],
+                    rhs=codes[("s", j)][:].bitcast(FP8X4),
+                    rhs_scale=scales[("s", j)][:],
+                    start=True,
+                    stop=True,
                 )
-            return g
+            acc[(w, j)] = ps
 
-        def quant(g, tag, bufs):
-            codes = work.tile([P, 512], U32, align_bytes=64, tag="c" + tag, bufs=bufs)
-            scl = work.tile([P, 512], U8, align_bytes=64, tag="s" + tag, bufs=bufs)
-            nc.vector.quantize_mx(out=codes[:].bitcast(FP8X4), scales=scl[:], in_=g[:])
-            return codes, scl
-
-        def prep_s(hs):
-            g = flip(s_sb[:].bitcast(F32)[:, 1024 * hs : 1024 * hs + 1024], nc.vector.tensor_copy)
-            s_codes[hs], s_scl[hs] = quant(g, "s", 2)
-
-        def prep_w(j):
-            for w in (1, 0):
-                g = flip(w_sb[w][j][:].bitcast(F32), nc.scalar.copy)
-                w_codes[(w, j)], w_scl[(w, j)] = quant(g, "w", 4)
-
-        def mx(j):
-            col = P * (j % 4)
-            for w in (1, 0):
-                ps = psx.tile([P, 512], F32, tag="mx")
-                for t in range(NT):
-                    nc.tensor.matmul_mx(
-                        out=ps[:, P * t : P * t + P],
-                        lhsT=w_codes[(w, j)][:, P * t : P * t + P].bitcast(FP8X4),
-                        lhsT_scale=w_scl[(w, j)][:, P * t : P * t + P],
-                        rhs=s_codes[j // 4][:, col : col + P].bitcast(FP8X4),
-                        rhs_scale=s_scl[j // 4][:, col : col + P],
-                        start=True,
-                        stop=True,
-                    )
-                acc[(w, j)] = ps
-
-        def epilogue(j):
+        def x_(j):
             e = work.tile([P, 512], F32, tag="e")
             for t in range(NT):
                 nc.scalar.activation(
                     out=e[:, P * t : P * t + P],
-                    in_=acc[(1, j)][:, P * t : P * t + P],
+                    in_=acc[(LS, j)][:, P * t : P * t + P],
                     func=ACT.Exp,
                     bias=bias[:, 16 * t + 8 + j : 16 * t + 9 + j],
                     scale=1.0,
                 )
+            sb[("e", j)] = e
+
+        def czo(j):
             a_sb = work.tile([P, 512], F32, tag="a")
             nc.vector.tensor_scalar(
-                out=a_sb[:], in0=e[:], scalar1=ebounds[:, 0:1], scalar2=ebounds[:, 1:2], op0=ALU.max, op1=ALU.min
+                out=a_sb[:],
+                in0=sb[("e", j)][:],
+                scalar1=ebounds[:, 0:1],
+                scalar2=ebounds[:, 1:2],
+                op0=ALU.max,
+                op1=ALU.min,
             )
             z = work.tile([P, 512], F32, tag="z")
             o = work.tile([P, 512], F32, tag="o")
@@ -178,40 +197,100 @@ def tile_skill_net_pa_kernel(tc, s, ei1, ej1, w11, b11, w12, b12, out):
             for t in range(NT):
                 nc.vector.scalar_tensor_tensor(
                     out=o[:, P * t : P * t + P],
-                    in0=acc[(0, j)][:, P * t : P * t + P],
+                    in0=acc[(MU, j)][:, P * t : P * t + P],
                     scalar=bias[:, 16 * t + j : 16 * t + j + 1],
                     in1=z[:, P * t : P * t + P],
                     op0=ALU.add,
                     op1=ALU.add,
                 )
-            o_sb[j] = o
+            sb[("o", j)] = o
 
-        def finish(j):
+        def ot_(j):
             ot = pso.tile([P, 512], F32, tag="ot")
             for t in range(NT):
-                nc.tensor.transpose(ot[:, P * t : P * t + P], o_sb[j][:, P * t : P * t + P], ident[:])
+                nc.tensor.transpose(ot[:, P * t : P * t + P], sb[("o", j)][:, P * t : P * t + P], ident[:])
+            banks[("o", j)] = ot
+
+        def r_(j):
             r = work.tile([P, 512], F32, tag="r", bufs=3)
             nc.scalar.activation(
-                out=r[:].rearrange("i (p t) -> i p t", t=NT), in_=ot[:].rearrange("i (t p) -> i p t", t=NT), func=ACT.Relu
+                out=r[:].rearrange("i (p t) -> i p t", t=NT),
+                in_=banks[("o", j)][:].rearrange("i (t p) -> i p t", t=NT),
+                func=ACT.Relu,
             )
             nc.sync.dma_start(out=out[:, j, :], in_=r[:])
 
-        def body():
-            prep_s(0)
-            prep_w(0)
-            for i in range(NM):
-                if i + 1 < NM:
-                    prep_w(i + 1)
-                if i == 2:
-                    prep_s(1)
-                if i >= 1:
-                    finish(i - 1)
-                mx(i)
-                epilogue(i)
-            finish(NM - 1)
+        vcopy = nc.vector.tensor_copy
+        scopy = nc.scalar.copy
 
-        if PIN:
-            with tc.manual_schedule():
-                body()
-        else:
-            body()
+        t_w(0, LS, 0)
+        t_w(0, LS, 1)
+        e_w(0, LS, 0, vcopy)
+        nc.vector.tensor_mul(out=f[:], in0=root[:], in1=sgn[:])
+        nc.gpsimd.tensor_scalar(
+            out=rep[:].rearrange("i (j c) -> i j c", j=NM),
+            in0=f[:, 32:40].unsqueeze(2).to_broadcast([P, NM, P]),
+            scalar1=1.0,
+            scalar2=0.0,
+            op0=ALU.mult,
+            op1=ALU.add,
+        )
+        e_w(0, LS, 1, vcopy)
+        t_s(0)
+        t_s(1)
+        e_s(0)
+        q_w(0, LS)
+        q_s(0)
+        e_s(1)
+        q_s(1)
+        t_w(0, MU, 0)
+        t_w(0, MU, 1)
+        e_w(0, MU, 0, scopy)
+        e_w(0, MU, 1, scopy)
+        for hh in range(2):
+            flip(("f", hh), rep[:, 512 * hh : 512 * hh + 512], 4)
+        for hh in range(2):
+            nc.vector.tensor_copy(out=fi_all[:, 512 * hh : 512 * hh + 512], in_=banks[("f", hh)][:])
+        q_w(0, MU)
+        t_w(1, LS, 0)
+        t_w(1, LS, 1)
+        mx(0, LS)
+        mx(0, MU)
+        t_w(1, MU, 0)
+        t_w(1, MU, 1)
+
+        for i in range(NM):
+            if i >= 1:
+                czo(i - 1)
+            if i + 1 < NM:
+                e_w(i + 1, LS, 0, scopy)
+                e_w(i + 1, LS, 1, scopy)
+            if i + 2 < NM:
+                t_w(i + 2, LS, 0)
+                t_w(i + 2, LS, 1)
+            if i + 1 < NM:
+                q_w(i + 1, LS)
+            if i >= 1:
+                ot_(i - 1)
+            if i + 1 < NM:
+                e_w(i + 1, MU, 0, scopy)
+            if i + 2 < NM:
+                t_s(i + 2)
+                e_s(i + 2)
+                q_s(i + 2)
+            if i + 1 < NM:
+                e_w(i + 1, MU, 1, scopy)
+            if i + 2 < NM:
+                t_w(i + 2, MU, 0)
+                t_w(i + 2, MU, 1)
+            if i + 1 < NM:
+                q_w(i + 1, MU)
+                mx(i + 1, LS)
+            x_(i)
+            if i + 1 < NM:
+                mx(i + 1, MU)
+            if i >= 1:
+                r_(i - 1)
+        czo(NM - 1)
+        ot_(NM - 1)
+        r_(NM - 1)

@@ -26,76 +26,36 @@ def tile_skill_net_pa_kernel(tc, s, ei1, ej1, w11, b11, w12, b12, out):
     ) as work, tc.psum_pool(name="pst", bufs=4) as pst, tc.psum_pool(name="psx", bufs=3) as psx, tc.psum_pool(
         name="pso", bufs=1
     ) as pso, tc.manual_schedule():
-        vecs = const.tile([P, H], BF16)
-        nc.vector.memset(vecs[:].bitcast(I32), 0)
-        ei_sb = const.tile([P, NM], BF16)
-        nc.scalar.dma_start(out=vecs[0:8, :], in_=b11)
-        nc.scalar.dma_start(out=vecs[8:16, :], in_=b12)
-        nc.scalar.dma_start(out=vecs[16:24, :], in_=ej1.rearrange("o j l -> (o j) l"))
-        nc.scalar.dma_start(out=ei_sb[:], in_=ei1.rearrange("i j o -> i (j o)"))
+        vcopy = nc.vector.tensor_copy
+        scopy = nc.scalar.copy
 
+        vecs = const.tile([P, H], BF16)
+        ei_sb = const.tile([P, NM], BF16)
+        zero_c = const.tile([P, 512], U32, align_bytes=64)
+        zero_s = const.tile([P, 512], U8, align_bytes=64)
+        zero_in = const.tile([P, 2048], BF16, align_bytes=64)
+        bounds = const.tile([P, 2], F32)
+        warm = const.tile([P, 1], F32)
+        ident = const.tile([P, P], F32)
+        vecf = const.tile([P, NT * P], F32)
+        bias = const.tile([P, NT * 16], F32)
+        ee = const.tile([P, 40], F32)
+        mag = const.tile([P, 40], F32)
+        neg = const.tile([P, 40], F32)
+        sgn = const.tile([P, 40], F32)
+        root = const.tile([P, 40], F32)
+        ebounds = const.tile([P, 2], F32)
+        f = const.tile([P, 40], F32)
+        rep = const.tile([P, NM * P], F32)
+        fi_all = const.tile([P, NM * P], F32)
+        s_codes = const.tile([P, NM * P], U32, align_bytes=64)
+        s_scales = const.tile([P, NM * P], U8, align_bytes=64)
         s_sb = raw.tile([P, NM * K], BF16)
-        s_flat = s.rearrange("i j k -> i (j k)")
         w_dram = {LS: w12, MU: w11}
         w_sb = {}
         for j in range(NM):
             for w in (LS, MU):
                 w_sb[(w, j)] = raw.tile([P, NT * K], BF16, name="w%d_%d" % (w, j))
-
-        def load_w(w, j, c0, c1):
-            nc.sync.dma_start(
-                out=w_sb[(w, j)][:, c0:c1], in_=w_dram[w][j].rearrange("(p t) k -> p (t k)", t=NT)[:, c0:c1]
-            )
-
-        def load_s(c):
-            nc.sync.dma_start(out=s_sb[:, 2 * K * c : 2 * K * (c + 1)], in_=s_flat[:, 2 * K * c : 2 * K * (c + 1)])
-
-        load_w(LS, 0, 0, 2 * K)
-        load_w(LS, 0, 2 * K, 4 * K)
-        load_s(0)
-        load_w(MU, 0, 0, 4 * K)
-        for j in range(1, NM):
-            load_w(LS, j, 0, 4 * K)
-            load_w(MU, j, 0, 4 * K)
-            if j % 2 == 1 and j < 7:
-                load_s((j + 1) // 2)
-
-        ident = const.tile([P, P], F32)
-        make_identity(nc, ident[:])
-
-        bounds = const.tile([P, 2], F32)
-        nc.vector.memset(bounds[:, 0:1], -20.0)
-        nc.vector.memset(bounds[:, 1:2], 4.0)
-        warm = const.tile([P, 1], F32)
-        nc.scalar.activation(out=warm[:], in_=bounds[:, 1:2], func=ACT.Sqrt)
-
-        vecf = const.tile([P, NT * P], F32)
-        nc.vector.tensor_copy(
-            out=vecf[:].rearrange("r (t p) -> r t p", t=NT), in_=vecs[:].rearrange("r (p t) -> r t p", t=NT)
-        )
-        vt = pst.tile([P, NT * P], F32, tag="tp")
-        for t in range(NT):
-            nc.tensor.transpose(vt[:, P * t : P * t + P], vecf[:, P * t : P * t + P], ident[:])
-        vt3 = vt[:].rearrange("p (t r) -> p t r", t=NT)
-        bias = const.tile([P, NT * 16], F32)
-        nc.vector.tensor_copy(out=bias[:].rearrange("p (t r) -> p t r", t=NT), in_=vt3[:, :, 0:16])
-        ee = const.tile([P, 40], F32)
-        nc.vector.tensor_copy(out=ee[:, 0:32].rearrange("p (t r) -> p t r", t=NT), in_=vt3[:, :, 16:24])
-        nc.vector.tensor_copy(out=ee[:, 32:40], in_=ei_sb[:])
-        mag = const.tile([P, 40], F32)
-        nc.vector.scalar_tensor_tensor(out=mag[:], in0=ee[:], scalar=-1.0, in1=ee[:], op0=ALU.mult, op1=ALU.max)
-        nc.vector.tensor_scalar_max(out=mag[:], in0=mag[:], scalar1=2.0 ** -116)
-        neg = const.tile([P, 40], F32)
-        nc.vector.tensor_single_scalar(out=neg[:], in_=ee[:], scalar=0.0, op=ALU.is_lt)
-        sgn = const.tile([P, 40], F32)
-        nc.vector.scalar_tensor_tensor(out=sgn[:], in0=ee[:], scalar=0.0, in1=neg[:], op0=ALU.is_gt, op1=ALU.subtract)
-        root = const.tile([P, 40], F32)
-        nc.scalar.activation(out=root[:], in_=mag[:], func=ACT.Sqrt)
-        ebounds = const.tile([P, 2], F32)
-        nc.scalar.activation(out=ebounds[:], in_=bounds[:], func=ACT.Exp)
-        f = const.tile([P, 40], F32)
-        rep = const.tile([P, NM * P], F32)
-        fi_all = const.tile([P, NM * P], F32)
 
         banks = {}
         grouped = {}
@@ -104,24 +64,32 @@ def tile_skill_net_pa_kernel(tc, s, ei1, ej1, w11, b11, w12, b12, out):
         acc = {}
         sb = {}
 
-        def flip(key, src32, n):
+        def load_w(w, j):
+            nc.sync.dma_start(out=w_sb[(w, j)][:], in_=w_dram[w][j].rearrange("(p t) k -> p (t k)", t=NT))
+
+        def load_s(c):
+            s_flat = s.rearrange("i j k -> i (j k)")
+            nc.sync.dma_start(out=s_sb[:, 2 * K * c : 2 * K * (c + 1)], in_=s_flat[:, 2 * K * c : 2 * K * (c + 1)])
+
+        def flip(key, src32):
             tp = pst.tile([P, 512], F32, tag="tp")
-            for a in range(n):
+            for a in range(4):
                 nc.tensor.transpose(tp[:, P * a : P * a + P], src32[:, P * a : P * a + P], ident[:])
             banks[key] = tp
 
+        def regroup(copy, dst32, key):
+            copy(
+                out=dst32.rearrange("q (a p u) -> q a p u", a=2, u=2),
+                in_=banks[key][:].rearrange("q (a u p) -> q a p u", a=2, u=2),
+            )
+
         def t_w(j, w, h):
-            flip((w, j, h), w_sb[(w, j)][:].bitcast(F32)[:, 512 * h : 512 * h + 512], 4)
+            flip((w, j, h), w_sb[(w, j)][:].bitcast(F32)[:, 512 * h : 512 * h + 512])
 
         def e_w(j, w, h, copy):
             if h == 0:
                 grouped[(w, j)] = work.tile([P, 2048], BF16, align_bytes=64, tag="g", bufs=4, name="g")
-            copy(
-                out=grouped[(w, j)][:].bitcast(F32)[:, 512 * h : 512 * h + 512].rearrange(
-                    "q (a p u) -> q a p u", a=2, u=2
-                ),
-                in_=banks[(w, j, h)][:].rearrange("q (a u p) -> q a p u", a=2, u=2),
-            )
+            regroup(copy, grouped[(w, j)][:].bitcast(F32)[:, 512 * h : 512 * h + 512], (w, j, h))
 
         def q_w(j, w):
             codes[(w, j)] = work.tile([P, 512], U32, align_bytes=64, tag="cw", bufs=4, name="cw")
@@ -130,36 +98,54 @@ def tile_skill_net_pa_kernel(tc, s, ei1, ej1, w11, b11, w12, b12, out):
                 out=codes[(w, j)][:].bitcast(FP8X4), scales=scales[(w, j)][:], in_=grouped[(w, j)][:]
             )
 
-        def t_s(j):
-            flip(("s", j), s_sb[:].bitcast(F32)[:, 256 * j : 256 * j + 256], 2)
+        def t_s(c):
+            flip(("s", c), s_sb[:].bitcast(F32)[:, 512 * c : 512 * c + 512])
 
-        def e_s(j):
-            grouped[("s", j)] = work.tile([P, 512], BF16, align_bytes=64, tag="gs", bufs=3, name="gs")
-            nc.vector.tensor_copy(
-                out=grouped[("s", j)][:].bitcast(F32).rearrange("q (p u) -> q p u", u=2),
-                in_=banks[("s", j)][:, 0:256].rearrange("q (u p) -> q p u", u=2),
-            )
+        def e_s(c, copy):
+            grouped[("s", c)] = work.tile([P, 1024], BF16, align_bytes=64, tag="gs", bufs=4, name="gs")
+            regroup(copy, grouped[("s", c)][:].bitcast(F32), ("s", c))
 
-        def q_s(j):
-            codes[("s", j)] = work.tile([P, P], U32, align_bytes=64, tag="cs", bufs=3, name="cs")
-            scales[("s", j)] = work.tile([P, P], U8, align_bytes=64, tag="ss", bufs=3, name="ss")
+        def q_s(c):
             nc.vector.quantize_mx(
-                out=codes[("s", j)][:].bitcast(FP8X4), scales=scales[("s", j)][:], in_=grouped[("s", j)][:]
+                out=s_codes[:, 256 * c : 256 * c + 256].bitcast(FP8X4),
+                scales=s_scales[:, 256 * c : 256 * c + 256],
+                in_=grouped[("s", c)][:],
             )
+
+        def dummy(ps, n):
+            for count in range(n):
+                nc.tensor.matmul_mx(
+                    out=ps[:],
+                    lhsT=zero_c[:, 0:P].bitcast(FP8X4),
+                    lhsT_scale=zero_s[:, 0:P],
+                    rhs=zero_c[:].bitcast(FP8X4),
+                    rhs_scale=zero_s[:],
+                    start=True,
+                    stop=True,
+                )
+
+        def open_bank(j, w):
+            acc[(w, j)] = psx.tile([P, 512], F32, tag="mx", name="mx")
+
+        def spare(n):
+            sp = pst.tile([P, 512], F32, tag="tp")
+            dummy(sp, n)
 
         def mx(j, w):
-            ps = psx.tile([P, 512], F32, tag="mx")
+            if (w, j) not in acc:
+                open_bank(j, w)
+            ps = acc[(w, j)]
+            dummy(ps, 1)
             for t in range(NT):
                 nc.tensor.matmul_mx(
                     out=ps[:, P * t : P * t + P],
                     lhsT=codes[(w, j)][:, P * t : P * t + P].bitcast(FP8X4),
                     lhsT_scale=scales[(w, j)][:, P * t : P * t + P],
-                    rhs=codes[("s", j)][:].bitcast(FP8X4),
-                    rhs_scale=scales[("s", j)][:],
+                    rhs=s_codes[:, P * j : P * j + P].bitcast(FP8X4),
+                    rhs_scale=s_scales[:, P * j : P * j + P],
                     start=True,
                     stop=True,
                 )
-            acc[(w, j)] = ps
 
         def x_(j):
             e = work.tile([P, 512], F32, tag="e")
@@ -220,12 +206,47 @@ def tile_skill_net_pa_kernel(tc, s, ei1, ej1, w11, b11, w12, b12, out):
             )
             nc.sync.dma_start(out=out[:, j, :], in_=r[:])
 
-        vcopy = nc.vector.tensor_copy
-        scopy = nc.scalar.copy
+        nc.vector.memset(vecs[:].bitcast(I32), 0)
+        nc.scalar.dma_start(out=vecs[0:8, :], in_=b11)
+        nc.scalar.dma_start(out=vecs[8:16, :], in_=b12)
+        nc.scalar.dma_start(out=vecs[16:24, :], in_=ej1.rearrange("o j l -> (o j) l"))
+        nc.scalar.dma_start(out=ei_sb[:], in_=ei1.rearrange("i j o -> i (j o)"))
+        load_s(0)
+        load_s(1)
+        load_w(LS, 0)
+        load_w(MU, 0)
+        load_s(2)
+        load_s(3)
+        for j in range(1, NM):
+            load_w(LS, j)
+            load_w(MU, j)
 
-        t_w(0, LS, 0)
-        t_w(0, LS, 1)
-        e_w(0, LS, 0, vcopy)
+        nc.vector.memset(zero_in[:].bitcast(I32), 0)
+        nc.vector.quantize_mx(out=zero_c[:].bitcast(FP8X4), scales=zero_s[:], in_=zero_in[:])
+        open_bank(0, LS)
+        dummy(acc[(LS, 0)], 6)
+        make_identity(nc, ident[:])
+        nc.vector.memset(bounds[:, 0:1], -20.0)
+        nc.vector.memset(bounds[:, 1:2], 4.0)
+        nc.scalar.activation(out=warm[:], in_=bounds[:, 1:2], func=ACT.Sqrt)
+
+        vcopy(out=vecf[:].rearrange("r (t p) -> r t p", t=NT), in_=vecs[:].rearrange("r (p t) -> r t p", t=NT))
+        flip("v", vecf[:])
+        vt3 = banks["v"][:].rearrange("p (t r) -> p t r", t=NT)
+        vcopy(out=bias[:].rearrange("p (t r) -> p t r", t=NT), in_=vt3[:, :, 0:16])
+        vcopy(out=ee[:, 0:32].rearrange("p (t r) -> p t r", t=NT), in_=vt3[:, :, 16:24])
+        vcopy(out=ee[:, 32:40], in_=ei_sb[:])
+        nc.vector.scalar_tensor_tensor(out=mag[:], in0=ee[:], scalar=-1.0, in1=ee[:], op0=ALU.mult, op1=ALU.max)
+        nc.vector.tensor_scalar_max(out=mag[:], in0=mag[:], scalar1=2.0 ** -116)
+        nc.vector.tensor_single_scalar(out=neg[:], in_=ee[:], scalar=0.0, op=ALU.is_lt)
+        nc.vector.scalar_tensor_tensor(out=sgn[:], in0=ee[:], scalar=0.0, in1=neg[:], op0=ALU.is_gt, op1=ALU.subtract)
+        nc.scalar.activation(out=root[:], in_=mag[:], func=ACT.Sqrt)
+        nc.scalar.activation(out=ebounds[:], in_=bounds[:], func=ACT.Exp)
+
+        t_s(0)
+        t_s(1)
+        dummy(acc[(LS, 0)], 2)
+        e_s(0, vcopy)
         nc.vector.tensor_mul(out=f[:], in0=root[:], in1=sgn[:])
         nc.gpsimd.tensor_scalar(
             out=rep[:].rearrange("i (j c) -> i j c", j=NM),
@@ -235,62 +256,72 @@ def tile_skill_net_pa_kernel(tc, s, ei1, ej1, w11, b11, w12, b12, out):
             op0=ALU.mult,
             op1=ALU.add,
         )
-        e_w(0, LS, 1, vcopy)
-        t_s(0)
-        t_s(1)
-        e_s(0)
-        q_w(0, LS)
+        e_s(1, vcopy)
+        t_w(0, LS, 0)
+        t_w(0, LS, 1)
         q_s(0)
-        e_s(1)
+        e_w(0, LS, 0, vcopy)
+        e_w(0, LS, 1, scopy)
         q_s(1)
+        for hh in range(2):
+            flip(("f", hh), rep[:, 512 * hh : 512 * hh + 512])
+        dummy(acc[(LS, 0)], 2)
+        q_w(0, LS)
+        vcopy(out=fi_all[:, 0:512], in_=banks[("f", 0)][:])
+        scopy(out=fi_all[:, 512:1024], in_=banks[("f", 1)][:])
         t_w(0, MU, 0)
         t_w(0, MU, 1)
-        e_w(0, MU, 0, scopy)
+        e_w(0, MU, 0, vcopy)
         e_w(0, MU, 1, scopy)
-        for hh in range(2):
-            flip(("f", hh), rep[:, 512 * hh : 512 * hh + 512], 4)
-        for hh in range(2):
-            nc.vector.tensor_copy(out=fi_all[:, 512 * hh : 512 * hh + 512], in_=banks[("f", hh)][:])
+        mx(0, LS)
+        t_s(2)
+        t_s(3)
         q_w(0, MU)
+        e_s(2, vcopy)
+        e_s(3, scopy)
         t_w(1, LS, 0)
         t_w(1, LS, 1)
-        mx(0, LS)
-        mx(0, MU)
+        open_bank(0, MU)
+        dummy(acc[(MU, 0)], 2)
+        q_s(2)
+        q_s(3)
         t_w(1, MU, 0)
         t_w(1, MU, 1)
 
         for i in range(NM):
+            last = i == NM - 1
+            j = i + 1
             if i >= 1:
                 czo(i - 1)
-            if i + 1 < NM:
-                e_w(i + 1, LS, 0, scopy)
-                e_w(i + 1, LS, 1, scopy)
-            if i + 2 < NM:
-                t_w(i + 2, LS, 0)
-                t_w(i + 2, LS, 1)
-            if i + 1 < NM:
-                q_w(i + 1, LS)
+            if last:
+                mx(i, MU)
+                spare(3)
+            if j < NM:
+                e_w(j, LS, 0, scopy)
+                e_w(j, LS, 1, scopy)
+            if j + 1 < NM:
+                t_w(j + 1, LS, 0)
+                t_w(j + 1, LS, 1)
+            if j < NM:
+                q_w(j, LS)
             if i >= 1:
                 ot_(i - 1)
-            if i + 1 < NM:
-                e_w(i + 1, MU, 0, scopy)
-            if i + 2 < NM:
-                t_s(i + 2)
-                e_s(i + 2)
-                q_s(i + 2)
-            if i + 1 < NM:
-                e_w(i + 1, MU, 1, scopy)
-            if i + 2 < NM:
-                t_w(i + 2, MU, 0)
-                t_w(i + 2, MU, 1)
-            if i + 1 < NM:
-                q_w(i + 1, MU)
-                mx(i + 1, LS)
+            if not last:
+                mx(i, MU)
+            if j < NM:
+                e_w(j, MU, 0, scopy)
+                e_w(j, MU, 1, vcopy if (j % 2 == 1) else scopy)
+            if j + 1 < NM:
+                t_w(j + 1, MU, 0)
+                t_w(j + 1, MU, 1)
+            if j < NM:
+                q_w(j, MU)
             x_(i)
-            if i + 1 < NM:
-                mx(i + 1, MU)
+            if j < NM:
+                mx(j, LS)
             if i >= 1:
                 r_(i - 1)
         czo(NM - 1)
+        spare(3)
         ot_(NM - 1)
         r_(NM - 1)

@@ -31,21 +31,19 @@ def tile_skill_net_pa_kernel(tc, s, ei1, ej1, w11, b11, w12, b12, out):
 
         vecs = const.tile([P, H], BF16)
         ei_sb = const.tile([P, NM], BF16)
+        zero_in = const.tile([P, 2048], BF16, align_bytes=64)
         zero_c = const.tile([P, 512], U32, align_bytes=64)
         zero_s = const.tile([P, 512], U8, align_bytes=64)
-        zero_in = const.tile([P, 2048], BF16, align_bytes=64)
         bounds = const.tile([P, 2], F32)
         warm = const.tile([P, 1], F32)
         ident = const.tile([P, P], F32)
         vecf = const.tile([P, NT * P], F32)
         bias = const.tile([P, NT * 16], F32)
-        ee = const.tile([P, 40], F32)
-        mag = const.tile([P, 40], F32)
-        neg = const.tile([P, 40], F32)
-        sgn = const.tile([P, 40], F32)
-        root = const.tile([P, 40], F32)
         ebounds = const.tile([P, 2], F32)
-        f = const.tile([P, 40], F32)
+        nz = {}
+        for kind, width in (("i", NM), ("j", NT * NM)):
+            for part in ("x", "mag", "neg", "sgn", "root", "f"):
+                nz[(kind, part)] = const.tile([P, width], F32, name="nz_%s_%s" % (kind, part))
         rep = const.tile([P, NM * P], F32)
         fi_all = const.tile([P, NM * P], F32)
         s_codes = const.tile([P, NM * P], U32, align_bytes=64)
@@ -131,11 +129,11 @@ def tile_skill_net_pa_kernel(tc, s, ei1, ej1, w11, b11, w12, b12, out):
             sp = pst.tile([P, 512], F32, tag="tp")
             dummy(sp, n)
 
-        def mx(j, w):
+        def mx(j, w, n_dummy):
             if (w, j) not in acc:
                 open_bank(j, w)
             ps = acc[(w, j)]
-            dummy(ps, 1)
+            dummy(ps, n_dummy)
             for t in range(NT):
                 nc.tensor.matmul_mx(
                     out=ps[:, P * t : P * t + P],
@@ -146,6 +144,23 @@ def tile_skill_net_pa_kernel(tc, s, ei1, ej1, w11, b11, w12, b12, out):
                     start=True,
                     stop=True,
                 )
+
+        def noise_a(kind):
+            x = nz[(kind, "x")]
+            nc.vector.scalar_tensor_tensor(
+                out=nz[(kind, "mag")][:], in0=x[:], scalar=-1.0, in1=x[:], op0=ALU.mult, op1=ALU.max
+            )
+            nc.vector.tensor_scalar_max(out=nz[(kind, "mag")][:], in0=nz[(kind, "mag")][:], scalar1=2.0 ** -116)
+            nc.vector.tensor_single_scalar(out=nz[(kind, "neg")][:], in_=x[:], scalar=0.0, op=ALU.is_lt)
+            nc.vector.scalar_tensor_tensor(
+                out=nz[(kind, "sgn")][:], in0=x[:], scalar=0.0, in1=nz[(kind, "neg")][:], op0=ALU.is_gt, op1=ALU.subtract
+            )
+
+        def noise_b(kind):
+            nc.scalar.activation(out=nz[(kind, "root")][:], in_=nz[(kind, "mag")][:], func=ACT.Sqrt)
+
+        def noise_c(kind):
+            nc.vector.tensor_mul(out=nz[(kind, "f")][:], in0=nz[(kind, "root")][:], in1=nz[(kind, "sgn")][:])
 
         def x_(j):
             e = work.tile([P, 512], F32, tag="e")
@@ -175,7 +190,7 @@ def tile_skill_net_pa_kernel(tc, s, ei1, ej1, w11, b11, w12, b12, out):
                 nc.vector.scalar_tensor_tensor(
                     out=z[:, P * t : P * t + P],
                     in0=a_sb[:, P * t : P * t + P],
-                    scalar=f[:, 8 * t + j : 8 * t + j + 1],
+                    scalar=nz[("j", "f")][:, 8 * t + j : 8 * t + j + 1],
                     in1=fi_all[:, P * j : P * j + P],
                     op0=ALU.mult,
                     op1=ALU.mult,
@@ -191,10 +206,19 @@ def tile_skill_net_pa_kernel(tc, s, ei1, ej1, w11, b11, w12, b12, out):
                 )
             sb[("o", j)] = o
 
-        def ot_(j):
+        def ot_(j, n_matmul):
             ot = pso.tile([P, 512], F32, tag="ot")
             for t in range(NT):
-                nc.tensor.transpose(ot[:, P * t : P * t + P], sb[("o", j)][:, P * t : P * t + P], ident[:])
+                if t < n_matmul:
+                    nc.tensor.matmul(
+                        out=ot[:, P * t : P * t + P],
+                        lhsT=sb[("o", j)][:, P * t : P * t + P],
+                        rhs=ident[:],
+                        start=True,
+                        stop=True,
+                    )
+                else:
+                    nc.tensor.transpose(ot[:, P * t : P * t + P], sb[("o", j)][:, P * t : P * t + P], ident[:])
             banks[("o", j)] = ot
 
         def r_(j):
@@ -207,10 +231,10 @@ def tile_skill_net_pa_kernel(tc, s, ei1, ej1, w11, b11, w12, b12, out):
             nc.sync.dma_start(out=out[:, j, :], in_=r[:])
 
         nc.vector.memset(vecs[:].bitcast(I32), 0)
+        nc.scalar.dma_start(out=ei_sb[:], in_=ei1.rearrange("i j o -> i (j o)"))
+        nc.scalar.dma_start(out=vecs[16:24, :], in_=ej1.rearrange("o j l -> (o j) l"))
         nc.scalar.dma_start(out=vecs[0:8, :], in_=b11)
         nc.scalar.dma_start(out=vecs[8:16, :], in_=b12)
-        nc.scalar.dma_start(out=vecs[16:24, :], in_=ej1.rearrange("o j l -> (o j) l"))
-        nc.scalar.dma_start(out=ei_sb[:], in_=ei1.rearrange("i j o -> i (j o)"))
         load_s(0)
         load_s(1)
         load_w(LS, 0)
@@ -230,53 +254,52 @@ def tile_skill_net_pa_kernel(tc, s, ei1, ej1, w11, b11, w12, b12, out):
         nc.vector.memset(bounds[:, 1:2], 4.0)
         nc.scalar.activation(out=warm[:], in_=bounds[:, 1:2], func=ACT.Sqrt)
 
-        vcopy(out=vecf[:].rearrange("r (t p) -> r t p", t=NT), in_=vecs[:].rearrange("r (p t) -> r t p", t=NT))
-        flip("v", vecf[:])
-        vt3 = banks["v"][:].rearrange("p (t r) -> p t r", t=NT)
-        vcopy(out=bias[:].rearrange("p (t r) -> p t r", t=NT), in_=vt3[:, :, 0:16])
-        vcopy(out=ee[:, 0:32].rearrange("p (t r) -> p t r", t=NT), in_=vt3[:, :, 16:24])
-        vcopy(out=ee[:, 32:40], in_=ei_sb[:])
-        nc.vector.scalar_tensor_tensor(out=mag[:], in0=ee[:], scalar=-1.0, in1=ee[:], op0=ALU.mult, op1=ALU.max)
-        nc.vector.tensor_scalar_max(out=mag[:], in0=mag[:], scalar1=2.0 ** -116)
-        nc.vector.tensor_single_scalar(out=neg[:], in_=ee[:], scalar=0.0, op=ALU.is_lt)
-        nc.vector.scalar_tensor_tensor(out=sgn[:], in0=ee[:], scalar=0.0, in1=neg[:], op0=ALU.is_gt, op1=ALU.subtract)
-        nc.scalar.activation(out=root[:], in_=mag[:], func=ACT.Sqrt)
-        nc.scalar.activation(out=ebounds[:], in_=bounds[:], func=ACT.Exp)
-
         t_s(0)
         t_s(1)
         dummy(acc[(LS, 0)], 2)
-        e_s(0, vcopy)
-        nc.vector.tensor_mul(out=f[:], in0=root[:], in1=sgn[:])
+        e_s(0, scopy)
+        e_s(1, vcopy)
+        vcopy(out=nz[("i", "x")][:], in_=ei_sb[:])
+        noise_a("i")
+        noise_b("i")
+        vcopy(out=vecf[:].rearrange("r (t p) -> r t p", t=NT), in_=vecs[:].rearrange("r (p t) -> r t p", t=NT))
+        noise_c("i")
         nc.gpsimd.tensor_scalar(
             out=rep[:].rearrange("i (j c) -> i j c", j=NM),
-            in0=f[:, 32:40].unsqueeze(2).to_broadcast([P, NM, P]),
+            in0=nz[("i", "f")][:].unsqueeze(2).to_broadcast([P, NM, P]),
             scalar1=1.0,
             scalar2=0.0,
             op0=ALU.mult,
             op1=ALU.add,
         )
-        e_s(1, vcopy)
+        q_s(0)
+        q_s(1)
         t_w(0, LS, 0)
         t_w(0, LS, 1)
-        q_s(0)
-        e_w(0, LS, 0, vcopy)
+        flip("v", vecf[:])
+        e_w(0, LS, 0, scopy)
         e_w(0, LS, 1, scopy)
-        q_s(1)
-        for hh in range(2):
-            flip(("f", hh), rep[:, 512 * hh : 512 * hh + 512])
+        vt3 = banks["v"][:].rearrange("p (t r) -> p t r", t=NT)
+        vcopy(out=bias[:].rearrange("p (t r) -> p t r", t=NT), in_=vt3[:, :, 0:16])
+        vcopy(out=nz[("j", "x")][:].rearrange("p (t r) -> p t r", t=NT), in_=vt3[:, :, 16:24])
+        noise_a("j")
         dummy(acc[(LS, 0)], 2)
-        q_w(0, LS)
-        vcopy(out=fi_all[:, 0:512], in_=banks[("f", 0)][:])
-        scopy(out=fi_all[:, 512:1024], in_=banks[("f", 1)][:])
         t_w(0, MU, 0)
         t_w(0, MU, 1)
-        e_w(0, MU, 0, vcopy)
-        e_w(0, MU, 1, scopy)
-        mx(0, LS)
+        q_w(0, LS)
+        e_w(0, MU, 0, scopy)
+        noise_b("j")
+        nc.scalar.activation(out=ebounds[:], in_=bounds[:], func=ACT.Exp)
+        e_w(0, MU, 1, vcopy)
+        noise_c("j")
+        for hh in range(2):
+            flip(("f", hh), rep[:, 512 * hh : 512 * hh + 512])
+        mx(0, LS, 1)
+        q_w(0, MU)
+        for hh in range(2):
+            vcopy(out=fi_all[:, 512 * hh : 512 * hh + 512], in_=banks[("f", hh)][:])
         t_s(2)
         t_s(3)
-        q_w(0, MU)
         e_s(2, vcopy)
         e_s(3, scopy)
         t_w(1, LS, 0)
@@ -294,8 +317,7 @@ def tile_skill_net_pa_kernel(tc, s, ei1, ej1, w11, b11, w12, b12, out):
             if i >= 1:
                 czo(i - 1)
             if last:
-                mx(i, MU)
-                spare(3)
+                mx(i, MU, 1)
             if j < NM:
                 e_w(j, LS, 0, scopy)
                 e_w(j, LS, 1, scopy)
@@ -305,23 +327,21 @@ def tile_skill_net_pa_kernel(tc, s, ei1, ej1, w11, b11, w12, b12, out):
             if j < NM:
                 q_w(j, LS)
             if i >= 1:
-                ot_(i - 1)
-            if not last:
-                mx(i, MU)
+                ot_(i - 1, 3)
             if j < NM:
                 e_w(j, MU, 0, scopy)
-                e_w(j, MU, 1, vcopy if (j % 2 == 1) else scopy)
+                e_w(j, MU, 1, vcopy if j % 2 == 1 else scopy)
             if j + 1 < NM:
                 t_w(j + 1, MU, 0)
                 t_w(j + 1, MU, 1)
             if j < NM:
                 q_w(j, MU)
+                mx(i, MU, 1)
+                mx(j, LS, 0)
             x_(i)
-            if j < NM:
-                mx(j, LS)
             if i >= 1:
                 r_(i - 1)
         czo(NM - 1)
         spare(3)
-        ot_(NM - 1)
+        ot_(NM - 1, 0)
         r_(NM - 1)

@@ -29,27 +29,28 @@ def tile_skill_net_pa_kernel(tc, s, ei1, ej1, w11, b11, w12, b12, out):
         vcopy = nc.vector.tensor_copy
         scopy = nc.scalar.copy
 
-        vecs = const.tile([P, H], BF16)
-        ei_sb = const.tile([P, NM], BF16)
+        NJ = NM * NT
+        noise_in = const.tile([P, NJ + NM], BF16)
+        b_sb = {MU: const.tile([P, NJ], BF16, name="b_mu"), LS: const.tile([P, NJ], BF16, name="b_ls")}
         zero_in = const.tile([P, 2048], BF16, align_bytes=64)
         zero_c = const.tile([P, 512], U32, align_bytes=64)
         zero_s = const.tile([P, 512], U8, align_bytes=64)
         bounds = const.tile([P, 2], F32)
         warm = const.tile([P, 1], F32)
         ident = const.tile([P, P], F32)
-        vecf = const.tile([P, NT * P], F32)
-        bias = const.tile([P, NT * 16], F32)
         ebounds = const.tile([P, 2], F32)
-        nz = {}
-        for kind, width in (("i", NM), ("j", NT * NM)):
-            for part in ("x", "mag", "neg", "sgn", "root", "f"):
-                nz[(kind, part)] = const.tile([P, width], F32, name="nz_%s_%s" % (kind, part))
+        mag = const.tile([P, NJ + NM], F32)
+        neg = const.tile([P, NJ + NM], F32)
+        sgn = const.tile([P, NJ + NM], F32)
+        root = const.tile([P, NJ + NM], F32)
+        f = const.tile([P, NJ + NM], F32)
         rep = const.tile([P, NM * P], F32)
         fi_all = const.tile([P, NM * P], F32)
         s_codes = const.tile([P, NM * P], U32, align_bytes=64)
         s_scales = const.tile([P, NM * P], U8, align_bytes=64)
         s_sb = raw.tile([P, NM * K], BF16)
         w_dram = {LS: w12, MU: w11}
+        b_dram = {LS: b12, MU: b11}
         w_sb = {}
         for j in range(NM):
             for w in (LS, MU):
@@ -62,12 +63,18 @@ def tile_skill_net_pa_kernel(tc, s, ei1, ej1, w11, b11, w12, b12, out):
         acc = {}
         sb = {}
 
-        def load_w(w, j):
-            nc.sync.dma_start(out=w_sb[(w, j)][:], in_=w_dram[w][j].rearrange("(p t) k -> p (t k)", t=NT))
+        def load_w(j):
+            for w in (LS, MU):
+                nc.sync.dma_start(out=w_sb[(w, j)][:], in_=w_dram[w][j].rearrange("(p t) k -> p (t k)", t=NT))
 
         def load_s(c):
             s_flat = s.rearrange("i j k -> i (j k)")
             nc.sync.dma_start(out=s_sb[:, 2 * K * c : 2 * K * (c + 1)], in_=s_flat[:, 2 * K * c : 2 * K * (c + 1)])
+
+        def load_b(w):
+            nc.sync.dma_start(
+                out=b_sb[w][:].rearrange("p (j t) -> p j t", t=NT), in_=b_dram[w].rearrange("j (p t) -> p j t", t=NT)
+            )
 
         def flip(key, src32):
             tp = pst.tile([P, 512], F32, tag="tp")
@@ -99,16 +106,20 @@ def tile_skill_net_pa_kernel(tc, s, ei1, ej1, w11, b11, w12, b12, out):
         def t_s(c):
             flip(("s", c), s_sb[:].bitcast(F32)[:, 512 * c : 512 * c + 512])
 
-        def e_s(c, copy):
-            grouped[("s", c)] = work.tile([P, 1024], BF16, align_bytes=64, tag="gs", bufs=4, name="gs")
-            regroup(copy, grouped[("s", c)][:].bitcast(F32), ("s", c))
-
-        def q_s(c):
+        def eq_s(c):
+            g = work.tile([P, 1024], BF16, align_bytes=64, tag="gs", bufs=2)
+            regroup(vcopy, g[:].bitcast(F32), ("s", c))
             nc.vector.quantize_mx(
                 out=s_codes[:, 256 * c : 256 * c + 256].bitcast(FP8X4),
                 scales=s_scales[:, 256 * c : 256 * c + 256],
-                in_=grouped[("s", c)][:],
+                in_=g[:],
             )
+
+        def t_f(hh):
+            flip(("f", hh), rep[:, 512 * hh : 512 * hh + 512])
+
+        def e_f(hh):
+            vcopy(out=fi_all[:, 512 * hh : 512 * hh + 512], in_=banks[("f", hh)][:])
 
         def dummy(ps, n):
             for count in range(n):
@@ -124,10 +135,6 @@ def tile_skill_net_pa_kernel(tc, s, ei1, ej1, w11, b11, w12, b12, out):
 
         def open_bank(j, w):
             acc[(w, j)] = psx.tile([P, 512], F32, tag="mx", name="mx")
-
-        def spare(n):
-            sp = pst.tile([P, 512], F32, tag="tp")
-            dummy(sp, n)
 
         def mx(j, w, n_dummy):
             if (w, j) not in acc:
@@ -145,23 +152,6 @@ def tile_skill_net_pa_kernel(tc, s, ei1, ej1, w11, b11, w12, b12, out):
                     stop=True,
                 )
 
-        def noise_a(kind):
-            x = nz[(kind, "x")]
-            nc.vector.scalar_tensor_tensor(
-                out=nz[(kind, "mag")][:], in0=x[:], scalar=-1.0, in1=x[:], op0=ALU.mult, op1=ALU.max
-            )
-            nc.vector.tensor_scalar_max(out=nz[(kind, "mag")][:], in0=nz[(kind, "mag")][:], scalar1=2.0 ** -116)
-            nc.vector.tensor_single_scalar(out=nz[(kind, "neg")][:], in_=x[:], scalar=0.0, op=ALU.is_lt)
-            nc.vector.scalar_tensor_tensor(
-                out=nz[(kind, "sgn")][:], in0=x[:], scalar=0.0, in1=nz[(kind, "neg")][:], op0=ALU.is_gt, op1=ALU.subtract
-            )
-
-        def noise_b(kind):
-            nc.scalar.activation(out=nz[(kind, "root")][:], in_=nz[(kind, "mag")][:], func=ACT.Sqrt)
-
-        def noise_c(kind):
-            nc.vector.tensor_mul(out=nz[(kind, "f")][:], in0=nz[(kind, "root")][:], in1=nz[(kind, "sgn")][:])
-
         def x_(j):
             e = work.tile([P, 512], F32, tag="e")
             for t in range(NT):
@@ -169,7 +159,7 @@ def tile_skill_net_pa_kernel(tc, s, ei1, ej1, w11, b11, w12, b12, out):
                     out=e[:, P * t : P * t + P],
                     in_=acc[(LS, j)][:, P * t : P * t + P],
                     func=ACT.Exp,
-                    bias=bias[:, 16 * t + 8 + j : 16 * t + 9 + j],
+                    bias=b_sb[LS][:, NT * j + t : NT * j + t + 1],
                     scale=1.0,
                 )
             sb[("e", j)] = e
@@ -190,7 +180,7 @@ def tile_skill_net_pa_kernel(tc, s, ei1, ej1, w11, b11, w12, b12, out):
                 nc.vector.scalar_tensor_tensor(
                     out=z[:, P * t : P * t + P],
                     in0=a_sb[:, P * t : P * t + P],
-                    scalar=nz[("j", "f")][:, 8 * t + j : 8 * t + j + 1],
+                    scalar=f[:, NT * j + t : NT * j + t + 1],
                     in1=fi_all[:, P * j : P * j + P],
                     op0=ALU.mult,
                     op1=ALU.mult,
@@ -199,15 +189,14 @@ def tile_skill_net_pa_kernel(tc, s, ei1, ej1, w11, b11, w12, b12, out):
                 nc.vector.scalar_tensor_tensor(
                     out=o[:, P * t : P * t + P],
                     in0=acc[(MU, j)][:, P * t : P * t + P],
-                    scalar=bias[:, 16 * t + j : 16 * t + j + 1],
+                    scalar=b_sb[MU][:, NT * j + t : NT * j + t + 1],
                     in1=z[:, P * t : P * t + P],
                     op0=ALU.add,
                     op1=ALU.add,
                 )
             sb[("o", j)] = o
 
-        def ot_(j, n_matmul):
-            ot = pso.tile([P, 512], F32, tag="ot")
+        def ot_(j, ot, n_matmul):
             for t in range(NT):
                 if t < n_matmul:
                     nc.tensor.matmul(
@@ -230,20 +219,23 @@ def tile_skill_net_pa_kernel(tc, s, ei1, ej1, w11, b11, w12, b12, out):
             )
             nc.sync.dma_start(out=out[:, j, :], in_=r[:])
 
-        nc.vector.memset(vecs[:].bitcast(I32), 0)
-        nc.scalar.dma_start(out=ei_sb[:], in_=ei1.rearrange("i j o -> i (j o)"))
-        nc.scalar.dma_start(out=vecs[16:24, :], in_=ej1.rearrange("o j l -> (o j) l"))
-        nc.scalar.dma_start(out=vecs[0:8, :], in_=b11)
-        nc.scalar.dma_start(out=vecs[8:16, :], in_=b12)
+        nc.sync.dma_start(
+            out=noise_in[:, 0:NJ].rearrange("p (j t) -> p j t", t=NT),
+            in_=ej1.rearrange("o j (p t) -> p (o j) t", t=NT),
+        )
+        nc.sync.dma_start(out=noise_in[:, NJ : NJ + NM], in_=ei1.rearrange("i j o -> i (j o)"))
         load_s(0)
+        load_w(0)
+        load_w(1)
+        load_b(LS)
         load_s(1)
-        load_w(LS, 0)
-        load_w(MU, 0)
+        load_w(2)
+        load_b(MU)
         load_s(2)
+        load_w(3)
         load_s(3)
-        for j in range(1, NM):
-            load_w(LS, j)
-            load_w(MU, j)
+        for j in range(4, NM):
+            load_w(j)
 
         nc.vector.memset(zero_in[:].bitcast(I32), 0)
         nc.vector.quantize_mx(out=zero_c[:].bitcast(FP8X4), scales=zero_s[:], in_=zero_in[:])
@@ -254,94 +246,97 @@ def tile_skill_net_pa_kernel(tc, s, ei1, ej1, w11, b11, w12, b12, out):
         nc.vector.memset(bounds[:, 1:2], 4.0)
         nc.scalar.activation(out=warm[:], in_=bounds[:, 1:2], func=ACT.Sqrt)
 
-        t_s(0)
-        t_s(1)
-        dummy(acc[(LS, 0)], 2)
-        e_s(0, scopy)
-        e_s(1, vcopy)
-        vcopy(out=nz[("i", "x")][:], in_=ei_sb[:])
-        noise_a("i")
-        noise_b("i")
-        vcopy(out=vecf[:].rearrange("r (t p) -> r t p", t=NT), in_=vecs[:].rearrange("r (p t) -> r t p", t=NT))
-        noise_c("i")
+        nc.vector.scalar_tensor_tensor(
+            out=mag[:], in0=noise_in[:], scalar=-1.0, in1=noise_in[:], op0=ALU.mult, op1=ALU.max
+        )
+        nc.vector.tensor_scalar_max(out=mag[:], in0=mag[:], scalar1=2.0 ** -116)
+        nc.vector.tensor_single_scalar(out=neg[:], in_=noise_in[:], scalar=0.0, op=ALU.is_lt)
+        nc.vector.scalar_tensor_tensor(
+            out=sgn[:], in0=noise_in[:], scalar=0.0, in1=neg[:], op0=ALU.is_gt, op1=ALU.subtract
+        )
+        nc.scalar.activation(out=root[:], in_=mag[:], func=ACT.Sqrt)
+        nc.scalar.activation(out=ebounds[:], in_=bounds[:], func=ACT.Exp)
+        nc.vector.tensor_mul(out=f[:], in0=root[:], in1=sgn[:])
         nc.gpsimd.tensor_scalar(
             out=rep[:].rearrange("i (j c) -> i j c", j=NM),
-            in0=nz[("i", "f")][:].unsqueeze(2).to_broadcast([P, NM, P]),
+            in0=f[:, NJ : NJ + NM].unsqueeze(2).to_broadcast([P, NM, P]),
             scalar1=1.0,
             scalar2=0.0,
             op0=ALU.mult,
             op1=ALU.add,
         )
-        q_s(0)
-        q_s(1)
+
+        t_s(0)
+        dummy(acc[(LS, 0)], 2)
+        eq_s(0)
         t_w(0, LS, 0)
         t_w(0, LS, 1)
-        flip("v", vecf[:])
         e_w(0, LS, 0, scopy)
-        e_w(0, LS, 1, scopy)
-        vt3 = banks["v"][:].rearrange("p (t r) -> p t r", t=NT)
-        vcopy(out=bias[:].rearrange("p (t r) -> p t r", t=NT), in_=vt3[:, :, 0:16])
-        vcopy(out=nz[("j", "x")][:].rearrange("p (t r) -> p t r", t=NT), in_=vt3[:, :, 16:24])
-        noise_a("j")
-        dummy(acc[(LS, 0)], 2)
+        e_w(0, LS, 1, vcopy)
         t_w(0, MU, 0)
         t_w(0, MU, 1)
+        dummy(acc[(LS, 0)], 2)
         q_w(0, LS)
         e_w(0, MU, 0, scopy)
-        noise_b("j")
-        nc.scalar.activation(out=ebounds[:], in_=bounds[:], func=ACT.Exp)
         e_w(0, MU, 1, vcopy)
-        noise_c("j")
-        for hh in range(2):
-            flip(("f", hh), rep[:, 512 * hh : 512 * hh + 512])
-        mx(0, LS, 1)
         q_w(0, MU)
-        for hh in range(2):
-            vcopy(out=fi_all[:, 512 * hh : 512 * hh + 512], in_=banks[("f", hh)][:])
-        t_s(2)
-        t_s(3)
-        e_s(2, vcopy)
-        e_s(3, scopy)
         t_w(1, LS, 0)
         t_w(1, LS, 1)
-        open_bank(0, MU)
-        dummy(acc[(MU, 0)], 2)
-        q_s(2)
-        q_s(3)
+        t_f(0)
+        e_f(0)
         t_w(1, MU, 0)
-        t_w(1, MU, 1)
 
-        for i in range(NM):
-            last = i == NM - 1
-            j = i + 1
-            if i >= 1:
-                czo(i - 1)
-            if last:
-                mx(i, MU, 1)
+        chores = {0: ("s", 1), 1: ("s", 2), 2: ("f", 1), 3: ("s", 3)}
+        for n in range(NM + 2):
+            j = n + 1
+            d = n - 1
+            chore = chores.get(n)
+            if n < NM:
+                mx(n, LS, 1)
+                mx(n, MU, 0)
+            if n == 0:
+                t_w(1, MU, 1)
+            if 0 <= d < NM:
+                czo(d)
             if j < NM:
                 e_w(j, LS, 0, scopy)
+            if n >= 2:
+                r_(n - 2)
+            if chore:
+                if chore[0] == "s":
+                    t_s(chore[1])
+                else:
+                    t_f(chore[1])
+            if j < NM:
                 e_w(j, LS, 1, scopy)
             if j + 1 < NM:
                 t_w(j + 1, LS, 0)
-                t_w(j + 1, LS, 1)
+            if chore:
+                if chore[0] == "s":
+                    eq_s(chore[1])
+                else:
+                    e_f(chore[1])
             if j < NM:
                 q_w(j, LS)
-            if i >= 1:
-                ot_(i - 1, 3)
-            if j < NM:
                 e_w(j, MU, 0, scopy)
-                e_w(j, MU, 1, vcopy if j % 2 == 1 else scopy)
+            if j + 1 < NM:
+                t_w(j + 1, LS, 1)
+            if j < NM:
+                e_w(j, MU, 1, scopy)
+            if 0 <= d < NM:
+                if d >= NM - 2:
+                    sp = pst.tile([P, 512], F32, tag="tp")
+                    dummy(sp, 2)
+                if d == NM - 1:
+                    last_ot = pst.tile([P, 512], F32, tag="tp")
+                    ot_(d, last_ot, 0)
+                else:
+                    ot = pso.tile([P, 512], F32, tag="ot")
+                    ot_(d, ot, 3)
             if j + 1 < NM:
                 t_w(j + 1, MU, 0)
                 t_w(j + 1, MU, 1)
             if j < NM:
                 q_w(j, MU)
-                mx(i, MU, 1)
-                mx(j, LS, 0)
-            x_(i)
-            if i >= 1:
-                r_(i - 1)
-        czo(NM - 1)
-        spare(3)
-        ot_(NM - 1, 0)
-        r_(NM - 1)
+            if n < NM:
+                x_(n)

@@ -32,9 +32,6 @@ def tile_skill_net_pa_kernel(tc, s, ei1, ej1, w11, b11, w12, b12, out):
         NJ = NM * NT
         noise_in = const.tile([P, NJ + NM], BF16)
         b_sb = {MU: const.tile([P, NJ], BF16, name="b_mu"), LS: const.tile([P, NJ], BF16, name="b_ls")}
-        zero_in = const.tile([P, 2048], BF16, align_bytes=64)
-        zero_c = const.tile([P, 512], U32, align_bytes=64)
-        zero_s = const.tile([P, 512], U8, align_bytes=64)
         bounds = const.tile([P, 2], F32)
         warm = const.tile([P, 1], F32)
         ident = const.tile([P, P], F32)
@@ -121,18 +118,6 @@ def tile_skill_net_pa_kernel(tc, s, ei1, ej1, w11, b11, w12, b12, out):
         def e_f(hh):
             vcopy(out=fi_all[:, 512 * hh : 512 * hh + 512], in_=banks[("f", hh)][:])
 
-        def dummy(ps, n):
-            for count in range(n):
-                nc.tensor.matmul_mx(
-                    out=ps[:],
-                    lhsT=zero_c[:, 0:P].bitcast(FP8X4),
-                    lhsT_scale=zero_s[:, 0:P],
-                    rhs=zero_c[:].bitcast(FP8X4),
-                    rhs_scale=zero_s[:],
-                    start=True,
-                    stop=True,
-                )
-
         def open_bank(j, w):
             acc[(w, j)] = psx.tile([P, 512], F32, tag="mx", name="mx")
 
@@ -140,7 +125,6 @@ def tile_skill_net_pa_kernel(tc, s, ei1, ej1, w11, b11, w12, b12, out):
             if (w, j) not in acc:
                 open_bank(j, w)
             ps = acc[(w, j)]
-            dummy(ps, n_dummy)
             for t in range(NT):
                 nc.tensor.matmul_mx(
                     out=ps[:, P * t : P * t + P],
@@ -237,10 +221,6 @@ def tile_skill_net_pa_kernel(tc, s, ei1, ej1, w11, b11, w12, b12, out):
         for j in range(4, NM):
             load_w(j)
 
-        nc.vector.memset(zero_in[:].bitcast(I32), 0)
-        nc.vector.quantize_mx(out=zero_c[:].bitcast(FP8X4), scales=zero_s[:], in_=zero_in[:])
-        open_bank(0, LS)
-        dummy(acc[(LS, 0)], 6)
         make_identity(nc, ident[:])
         nc.vector.memset(bounds[:, 0:1], -20.0)
         nc.vector.memset(bounds[:, 1:2], 4.0)
@@ -267,7 +247,6 @@ def tile_skill_net_pa_kernel(tc, s, ei1, ej1, w11, b11, w12, b12, out):
         )
 
         t_s(0)
-        dummy(acc[(LS, 0)], 2)
         eq_s(0)
         t_w(0, LS, 0)
         t_w(0, LS, 1)
@@ -275,7 +254,6 @@ def tile_skill_net_pa_kernel(tc, s, ei1, ej1, w11, b11, w12, b12, out):
         e_w(0, LS, 1, vcopy)
         t_w(0, MU, 0)
         t_w(0, MU, 1)
-        dummy(acc[(LS, 0)], 2)
         q_w(0, LS)
         e_w(0, MU, 0, scopy)
         e_w(0, MU, 1, vcopy)
@@ -292,7 +270,7 @@ def tile_skill_net_pa_kernel(tc, s, ei1, ej1, w11, b11, w12, b12, out):
             d = n - 1
             chore = chores.get(n)
             if n < NM:
-                mx(n, LS, 1)
+                mx(n, LS, 0)
                 mx(n, MU, 0)
             if n == 0:
                 t_w(1, MU, 1)
@@ -324,15 +302,12 @@ def tile_skill_net_pa_kernel(tc, s, ei1, ej1, w11, b11, w12, b12, out):
             if j < NM:
                 e_w(j, MU, 1, scopy)
             if 0 <= d < NM:
-                if d >= NM - 2:
-                    sp = pst.tile([P, 512], F32, tag="tp")
-                    dummy(sp, 2)
                 if d == NM - 1:
                     last_ot = pst.tile([P, 512], F32, tag="tp")
                     ot_(d, last_ot, 0)
                 else:
                     ot = pso.tile([P, 512], F32, tag="ot")
-                    ot_(d, ot, 3)
+                    ot_(d, ot, 0)
             if j + 1 < NM:
                 t_w(j + 1, MU, 0)
                 t_w(j + 1, MU, 1)

@@ -25,7 +25,7 @@ def tile_skill_net_pa_kernel(tc, s, ei1, ej1, w11, b11, w12, b12, out):
         name="work", bufs=2
     ) as work, tc.psum_pool(name="pst", bufs=4) as pst, tc.psum_pool(name="psx", bufs=3) as psx, tc.psum_pool(
         name="pso", bufs=1
-    ) as pso, tc.manual_schedule():
+    ) as pso:
         vcopy = nc.vector.tensor_copy
         scopy = nc.scalar.copy
 
@@ -221,30 +221,31 @@ def tile_skill_net_pa_kernel(tc, s, ei1, ej1, w11, b11, w12, b12, out):
         for j in range(4, NM):
             load_w(j)
 
-        make_identity(nc, ident[:])
-        nc.vector.memset(bounds[:, 0:1], -20.0)
-        nc.vector.memset(bounds[:, 1:2], 4.0)
-        nc.scalar.activation(out=warm[:], in_=bounds[:, 1:2], func=ACT.Sqrt)
+        with tc.manual_schedule():
+            make_identity(nc, ident[:])
+            nc.vector.memset(bounds[:, 0:1], -20.0)
+            nc.vector.memset(bounds[:, 1:2], 4.0)
+            nc.scalar.activation(out=warm[:], in_=bounds[:, 1:2], func=ACT.Sqrt)
 
-        nc.vector.scalar_tensor_tensor(
-            out=mag[:], in0=noise_in[:], scalar=-1.0, in1=noise_in[:], op0=ALU.mult, op1=ALU.max
-        )
-        nc.vector.tensor_scalar_max(out=mag[:], in0=mag[:], scalar1=2.0 ** -116)
-        nc.vector.tensor_single_scalar(out=neg[:], in_=noise_in[:], scalar=0.0, op=ALU.is_lt)
-        nc.vector.scalar_tensor_tensor(
-            out=sgn[:], in0=noise_in[:], scalar=0.0, in1=neg[:], op0=ALU.is_gt, op1=ALU.subtract
-        )
-        nc.scalar.activation(out=root[:], in_=mag[:], func=ACT.Sqrt)
-        nc.scalar.activation(out=ebounds[:], in_=bounds[:], func=ACT.Exp)
-        nc.vector.tensor_mul(out=f[:], in0=root[:], in1=sgn[:])
-        nc.gpsimd.tensor_scalar(
-            out=rep[:].rearrange("i (j c) -> i j c", j=NM),
-            in0=f[:, NJ : NJ + NM].unsqueeze(2).to_broadcast([P, NM, P]),
-            scalar1=1.0,
-            scalar2=0.0,
-            op0=ALU.mult,
-            op1=ALU.add,
-        )
+            nc.vector.scalar_tensor_tensor(
+                out=mag[:], in0=noise_in[:], scalar=-1.0, in1=noise_in[:], op0=ALU.mult, op1=ALU.max
+            )
+            nc.vector.tensor_scalar_max(out=mag[:], in0=mag[:], scalar1=2.0 ** -116)
+            nc.vector.tensor_single_scalar(out=neg[:], in_=noise_in[:], scalar=0.0, op=ALU.is_lt)
+            nc.vector.scalar_tensor_tensor(
+                out=sgn[:], in0=noise_in[:], scalar=0.0, in1=neg[:], op0=ALU.is_gt, op1=ALU.subtract
+            )
+            nc.scalar.activation(out=root[:], in_=mag[:], func=ACT.Sqrt)
+            nc.scalar.activation(out=ebounds[:], in_=bounds[:], func=ACT.Exp)
+            nc.vector.tensor_mul(out=f[:], in0=root[:], in1=sgn[:])
+            nc.gpsimd.tensor_scalar(
+                out=rep[:].rearrange("i (j c) -> i j c", j=NM),
+                in0=f[:, NJ : NJ + NM].unsqueeze(2).to_broadcast([P, NM, P]),
+                scalar1=1.0,
+                scalar2=0.0,
+                op0=ALU.mult,
+                op1=ALU.add,
+            )
 
         t_s(0)
         eq_s(0)

@@ -308,7 +308,7 @@ def tile_skill_net_pa_kernel(tc, s, ei1, ej1, w11, b11, w12, b12, out):
                     ot_(d, last_ot, 0)
                 else:
                     ot = pso.tile([P, 512], F32, tag="ot")
-                    ot_(d, ot, 0)
+                    ot_(d, ot, 3)
             if j + 1 < NM:
                 t_w(j + 1, MU, 0)
                 t_w(j + 1, MU, 1)

import concourse.mybir as mybir
from concourse.masks import make_identity

F32 = mybir.dt.float32
BF16 = mybir.dt.bfloat16
U32 = mybir.dt.uint32
U8 = mybir.dt.uint8
I32 = mybir.dt.int32
FP8X4 = mybir.dt.float8_e4m3fn_x4
ALU = mybir.AluOpType
ACT = mybir.ActivationFunctionType

P = 128
NM = 8
K = 512
H = 512
NT = H // P
FLOPS = 2 * 2 * P * NM * K * H
LS, MU = 1, 0


def tile_skill_net_pa_kernel(tc, s, ei1, ej1, w11, b11, w12, b12, out):
    nc = tc.nc
    with tc.tile_pool(name="const", bufs=1) as const, tc.tile_pool(name="raw", bufs=1) as raw, tc.tile_pool(
        name="work", bufs=2
    ) as work, tc.psum_pool(name="pst", bufs=4) as pst, tc.psum_pool(name="psx", bufs=3) as psx, tc.psum_pool(
        name="pso", bufs=1
    ) as pso:
        vcopy = nc.vector.tensor_copy
        scopy = nc.scalar.copy

        NJ = NM * NT
        noise_in = const.tile([P, NJ + NM], BF16)
        b_sb = {MU: const.tile([P, NJ], BF16, name="b_mu"), LS: const.tile([P, NJ], BF16, name="b_ls")}
        bounds = const.tile([P, 2], F32)
        warm = const.tile([P, 1], F32)
        ident = const.tile([P, P], F32)
        ebounds = const.tile([P, 2], F32)
        mag = const.tile([P, NJ + NM], F32)
        neg = const.tile([P, NJ + NM], F32)
        sgn = const.tile([P, NJ + NM], F32)
        root = const.tile([P, NJ + NM], F32)
        f = const.tile([P, NJ + NM], F32)
        rep = const.tile([P, NM * P], F32)
        fi_all = const.tile([P, NM * P], F32)
        s_codes = const.tile([P, NM * P], U32, align_bytes=64)
        s_scales = const.tile([P, NM * P], U8, align_bytes=64)
        s_sb = raw.tile([P, NM * K], BF16)
        w_dram = {LS: w12, MU: w11}
        b_dram = {LS: b12, MU: b11}
        w_sb = {}
        for j in range(NM):
            for w in (LS, MU):
                w_sb[(w, j)] = raw.tile([P, NT * K], BF16, name="w%d_%d" % (w, j))

        banks = {}
        grouped = {}
        codes = {}
        scales = {}
        acc = {}
        sb = {}

        def load_w(j):
            for w in (LS, MU):
                nc.sync.dma_start(out=w_sb[(w, j)][:], in_=w_dram[w][j].rearrange("(p t) k -> p (t k)", t=NT))

        def load_s(c):
            s_flat = s.rearrange("i j k -> i (j k)")
            nc.sync.dma_start(out=s_sb[:, 2 * K * c : 2 * K * (c + 1)], in_=s_flat[:, 2 * K * c : 2 * K * (c + 1)])

        def load_b(w):
            nc.sync.dma_start(
                out=b_sb[w][:].rearrange("p (j t) -> p j t", t=NT), in_=b_dram[w].rearrange("j (p t) -> p j t", t=NT)
            )

        def flip(key, src32):
            tp = pst.tile([P, 512], F32, tag="tp")
            for a in range(4):
                nc.tensor.transpose(tp[:, P * a : P * a + P], src32[:, P * a : P * a + P], ident[:])
            banks[key] = tp

        def regroup(copy, dst32, key):
            copy(
                out=dst32.rearrange("q (a p u) -> q a p u", a=2, u=2),
                in_=banks[key][:].rearrange("q (a u p) -> q a p u", a=2, u=2),
            )

        def t_w(j, w, h):
            flip((w, j, h), w_sb[(w, j)][:].bitcast(F32)[:, 512 * h : 512 * h + 512])

        def e_w(j, w, h, copy):
            if h == 0:
                grouped[(w, j)] = work.tile([P, 2048], BF16, align_bytes=64, tag="g", bufs=4, name="g")
            regroup(copy, grouped[(w, j)][:].bitcast(F32)[:, 512 * h : 512 * h + 512], (w, j, h))

        def q_w(j, w):
            codes[(w, j)] = work.tile([P, 512], U32, align_bytes=64, tag="cw", bufs=4, name="cw")
            scales[(w, j)] = work.tile([P, 512], U8, align_bytes=64, tag="sw", bufs=4, name="sw")
            nc.vector.quantize_mx(
                out=codes[(w, j)][:].bitcast(FP8X4), scales=scales[(w, j)][:], in_=grouped[(w, j)][:]
            )

        def t_s(c):
            flip(("s", c), s_sb[:].bitcast(F32)[:, 512 * c : 512 * c + 512])

        def eq_s(c):
            g = work.tile([P, 1024], BF16, align_bytes=64, tag="gs", bufs=2)
            regroup(vcopy, g[:].bitcast(F32), ("s", c))
            nc.vector.quantize_mx(
                out=s_codes[:, 256 * c : 256 * c + 256].bitcast(FP8X4),
                scales=s_scales[:, 256 * c : 256 * c + 256],
                in_=g[:],
            )

        def t_f(hh):
            flip(("f", hh), rep[:, 512 * hh : 512 * hh + 512])

        def e_f(hh):
            vcopy(out=fi_all[:, 512 * hh : 512 * hh + 512], in_=banks[("f", hh)][:])

        def open_bank(j, w):
            acc[(w, j)] = psx.tile([P, 512], F32, tag="mx", name="mx")

        def mx(j, w, n_dummy):
            if (w, j) not in acc:
                open_bank(j, w)
            ps = acc[(w, j)]
            for t in range(NT):
                nc.tensor.matmul_mx(
                    out=ps[:, P * t : P * t + P],
                    lhsT=codes[(w, j)][:, P * t : P * t + P].bitcast(FP8X4),
                    lhsT_scale=scales[(w, j)][:, P * t : P * t + P],
                    rhs=s_codes[:, P * j : P * j + P].bitcast(FP8X4),
                    rhs_scale=s_scales[:, P * j : P * j + P],
                    start=True,
                    stop=True,
                )

        def x_(j):
            e = work.tile([P, 512], F32, tag="e")
            for t in range(NT):
                nc.scalar.activation(
                    out=e[:, P * t : P * t + P],
                    in_=acc[(LS, j)][:, P * t : P * t + P],
                    func=ACT.Exp,
                    bias=b_sb[LS][:, NT * j + t : NT * j + t + 1],
                    scale=1.0,
                )
            sb[("e", j)] = e

        def czo(j):
            a_sb = work.tile([P, 512], F32, tag="a")
            nc.vector.tensor_scalar(
                out=a_sb[:],
                in0=sb[("e", j)][:],
                scalar1=ebounds[:, 0:1],
                scalar2=ebounds[:, 1:2],
                op0=ALU.max,
                op1=ALU.min,
            )
            z = work.tile([P, 512], F32, tag="z")
            o = work.tile([P, 512], F32, tag="o")
            for t in range(NT):
                nc.vector.scalar_tensor_tensor(
                    out=z[:, P * t : P * t + P],
                    in0=a_sb[:, P * t : P * t + P],
                    scalar=f[:, NT * j + t : NT * j + t + 1],
                    in1=fi_all[:, P * j : P * j + P],
                    op0=ALU.mult,
                    op1=ALU.mult,
                )
            for t in range(NT):
                nc.vector.scalar_tensor_tensor(
                    out=o[:, P * t : P * t + P],
                    in0=acc[(MU, j)][:, P * t : P * t + P],
                    scalar=b_sb[MU][:, NT * j + t : NT * j + t + 1],
                    in1=z[:, P * t : P * t + P],
                    op0=ALU.add,
                    op1=ALU.add,
                )
            sb[("o", j)] = o

        def ot_(j, ot, n_matmul):
            for t in range(NT):
                if t < n_matmul:
                    nc.tensor.matmul(
                        out=ot[:, P * t : P * t + P],
                        lhsT=sb[("o", j)][:, P * t : P * t + P],
                        rhs=ident[:],
                        start=True,
                        stop=True,
                    )
                else:
                    nc.tensor.transpose(ot[:, P * t : P * t + P], sb[("o", j)][:, P * t : P * t + P], ident[:])
            banks[("o", j)] = ot

        def r_(j):
            r = work.tile([P, 512], F32, tag="r", bufs=3)
            nc.scalar.activation(
                out=r[:].rearrange("i (p t) -> i p t", t=NT),
                in_=banks[("o", j)][:].rearrange("i (t p) -> i p t", t=NT),
                func=ACT.Relu,
            )
            nc.sync.dma_start(out=out[:, j, :], in_=r[:])

        nc.sync.dma_start(
            out=noise_in[:, 0:NJ].rearrange("p (j t) -> p j t", t=NT),
            in_=ej1.rearrange("o j (p t) -> p (o j) t", t=NT),
        )
        nc.sync.dma_start(out=noise_in[:, NJ : NJ + NM], in_=ei1.rearrange("i j o -> i (j o)"))
        load_s(0)
        load_w(0)
        load_w(1)
        load_b(LS)
        load_s(1)
        load_w(2)
        load_b(MU)
        load_s(2)
        load_w(3)
        load_s(3)
        for j in range(4, NM):
            load_w(j)

        with tc.manual_schedule():
            make_identity(nc, ident[:])
            nc.vector.memset(bounds[:, 0:1], -20.0)
            nc.vector.memset(bounds[:, 1:2], 4.0)
            nc.scalar.activation(out=warm[:], in_=bounds[:, 1:2], func=ACT.Sqrt)

            nc.vector.scalar_tensor_tensor(
                out=mag[:], in0=noise_in[:], scalar=-1.0, in1=noise_in[:], op0=ALU.mult, op1=ALU.max
            )
            nc.vector.tensor_scalar_max(out=mag[:], in0=mag[:], scalar1=2.0 ** -116)
            nc.vector.tensor_single_scalar(out=neg[:], in_=noise_in[:], scalar=0.0, op=ALU.is_lt)
            nc.vector.scalar_tensor_tensor(
                out=sgn[:], in0=noise_in[:], scalar=0.0, in1=neg[:], op0=ALU.is_gt, op1=ALU.subtract
            )
            nc.scalar.activation(out=root[:], in_=mag[:], func=ACT.Sqrt)
            nc.scalar.activation(out=ebounds[:], in_=bounds[:], func=ACT.Exp)
            nc.vector.tensor_mul(out=f[:], in0=root[:], in1=sgn[:])
            nc.gpsimd.tensor_scalar(
                out=rep[:].rearrange("i (j c) -> i j c", j=NM),
                in0=f[:, NJ : NJ + NM].unsqueeze(2).to_broadcast([P, NM, P]),
                scalar1=1.0,
                scalar2=0.0,
                op0=ALU.mult,
                op1=ALU.add,
            )

        t_s(0)
        eq_s(0)
        t_w(0, LS, 0)
        t_w(0, LS, 1)
        e_w(0, LS, 0, scopy)
        e_w(0, LS, 1, vcopy)
        t_w(0, MU, 0)
        t_w(0, MU, 1)
        q_w(0, LS)
        e_w(0, MU, 0, scopy)
        e_w(0, MU, 1, vcopy)
        q_w(0, MU)
        t_w(1, LS, 0)
        t_w(1, LS, 1)
        t_f(0)
        e_f(0)
        t_w(1, MU, 0)

        chores = {0: ("s", 1), 1: ("s", 2), 2: ("f", 1), 3: ("s", 3)}
        for n in range(NM + 2):
            j = n + 1
            d = n - 1
            chore = chores.get(n)
            if n < NM:
                mx(n, LS, 0)
                mx(n, MU, 0)
            if n == 0:
                t_w(1, MU, 1)
            if 0 <= d < NM:
                czo(d)
            if j < NM:
                e_w(j, LS, 0, scopy)
            if n >= 2:
                r_(n - 2)
            if chore:
                if chore[0] == "s":
                    t_s(chore[1])
                else:
                    t_f(chore[1])
            if j < NM:
                e_w(j, LS, 1, scopy)
            if j + 1 < NM:
                t_w(j + 1, LS, 0)
            if chore:
                if chore[0] == "s":
                    eq_s(chore[1])
                else:
                    e_f(chore[1])
            if j < NM:
                q_w(j, LS)
                e_w(j, MU, 0, scopy)
            if j + 1 < NM:
                t_w(j + 1, LS, 1)
            if j < NM:
                e_w(j, MU, 1, scopy)
            if 0 <= d < NM:
                if d == NM - 1:
                    last_ot = pst.tile([P, 512], F32, tag="tp")
                    ot_(d, last_ot, 0)
                else:
                    ot = pso.tile([P, 512], F32, tag="ot")
                    ot_(d, ot, 3)
            if j + 1 < NM:
                t_w(j + 1, MU, 0)
                t_w(j + 1, MU, 1)
            if j < NM:
                q_w(j, MU)
            if n < NM:
                x_(n)
